import numpy as np
import ml_dtypes


def mxq(x, axis, fmt="e4m3"):
    dtype, down = {"e4m3": (ml_dtypes.float8_e4m3fn, 7), "e5m2": (ml_dtypes.float8_e5m2, 14)}[fmt]
    v = np.moveaxis(np.asarray(x, np.float32).astype(ml_dtypes.bfloat16).astype(np.float64), axis, -1)
    blocks = v.reshape(v.shape[:-1] + (-1, 32))
    amax = np.abs(blocks).max(-1, keepdims=True)
    byte = np.maximum(np.where(amax > 0, np.frexp(amax)[1] - 1 + 127, 0) - down, 1)
    scale = np.exp2(byte - 127.0)
    codes = (blocks / scale).astype(np.float32).astype(dtype).astype(np.float64)
    return np.moveaxis((codes * scale).reshape(v.shape), -1, axis)


WIDE = False


def mx_kscale(k):
    if not WIDE:
        return np.ones(k)
    levels = np.array([10, -10, 5, -5, 0])
    a = np.random.permutation(np.resize(levels, k // 512 * 4)).reshape(k // 512, 4)
    idx = np.arange(k)
    return np.exp2(a[idx // 512, idx % 128 // 32])


BF16 = ml_dtypes.bfloat16


def bf(x):
    return np.asarray(x, np.float32).astype(BF16)


def f64(x):
    return np.asarray(x).astype(np.float64)


N, IN_CH, OUT_CH = 4096, 128, 128


def setup_inputs():
    t = mx_kscale(N)
    w = t.max() / t
    g = w.mean()
    a = 1.0 / (1.0 + N * np.random.random((N, N)))
    return {"x": bf(np.random.standard_normal((N, IN_CH)) * 2.0 * (g / w)[:, None]),
            "edge_index": bf(a * w),
            "weight": bf(np.random.standard_normal((IN_CH, OUT_CH)) * 2.0 / np.sqrt(IN_CH)),
            "bias": bf(np.random.standard_normal(OUT_CH) * 0.2)}


def reference(x, edge_index, weight, bias):
    adj = f64(edge_index) + np.eye(edge_index.shape[0])
    adj_sq = np.square(adj)
    row_sum = adj.sum(axis=-1)
    denom = np.square(row_sum) - adj_sq.sum(axis=-1)
    with np.errstate(divide="ignore"):
        norm = 1.0 / denom
    norm = np.where(np.isinf(norm), 0.0, norm)
    xw = f64(x) @ f64(weight)
    s = mxq(adj, 1, "e4m3") @ mxq(xw, 0, "e4m3")
    out = np.square(s) - (mxq(adj_sq, 1, "e4m3") @ mxq(np.square(xw), 0, "e4m3"))
    return norm[:, None] * out + f64(bias)

@@ -1,0 +1,283 @@
+from contextlib import ExitStack
+
+import concourse.mybir as mybir
+from concourse.masks import make_identity
+
+F32 = mybir.dt.float32
+BF16 = mybir.dt.bfloat16
+U32 = mybir.dt.uint32
+U8 = mybir.dt.uint8
+FP8X4 = mybir.dt.float8_e4m3fn_x4
+ALU = mybir.AluOpType
+ACT = mybir.ActivationFunctionType
+AX = mybir.AxisListType
+
+P = 128
+N = 4096
+C = 128
+NT = N // P
+NG = N // 512
+FLOPS = 2 * N * N * C * 2 + 2 * N * C * C
+
+
+def tile_bgnna_kernel(tc, x, edge_index, weight, bias, out):
+    nc = tc.nc
+    with ExitStack() as ctx:
+        const = ctx.enter_context(tc.tile_pool(name="const", bufs=1))
+        epool = ctx.enter_context(tc.tile_pool(name="epool", bufs=4))
+        gpool = ctx.enter_context(tc.tile_pool(name="gpool", bufs=2))
+        cpool = ctx.enter_context(tc.tile_pool(name="cpool", bufs=2))
+        work = ctx.enter_context(tc.tile_pool(name="work", bufs=2))
+        tpsum = ctx.enter_context(tc.psum_pool(name="tpsum", bufs=4))
+        apsum = ctx.enter_context(tc.psum_pool(name="apsum", bufs=1))
+
+        ident_f = const.tile([P, P], F32)
+        make_identity(nc, ident_f[:])
+        ident_b = const.tile([P, P], BF16)
+        make_identity(nc, ident_b[:])
+        ones_b = const.tile([P, 2], BF16)
+        nc.vector.memset(ones_b[:], 1.0)
+
+        mask = const.tile([P, 4, 512], BF16)
+        nc.vector.memset(mask[:], 0.0)
+        for v in range(4):
+            u_t, par = v // 2, v % 2
+            mv = mask[:, v, :].rearrange("p (h e t) -> p h e t", h=64, e=2, t=4)
+            for e in range(2):
+                nc.vector.tensor_copy(out=mv[:, :, e, 2 * u_t + e], in_=ident_b[:, 64 * par : 64 * par + 64])
+
+        gsel = const.tile([P, 32], F32)
+        nc.vector.tensor_reduce(out=gsel[:], in_=ident_f[:].rearrange("p (c t) -> p c t", t=4), axis=AX.X, op=ALU.add)
+        fold = const.tile([P, 4, P], F32)
+        nc.vector.memset(fold[:], 0.0)
+        for sub in range(4):
+            nc.vector.tensor_copy(out=fold[:, sub, 32 * sub : 32 * sub + 32], in_=gsel[:])
+
+        x_sb = const.tile([P, N], BF16)
+        nc.sync.dma_start(
+            out=x_sb[:].rearrange("q (a r) -> q a r", a=16),
+            in_=x.rearrange("(a q e) i -> q a (e i)", a=16, q=P, e=2),
+        )
+        w_sb = const.tile([P, C], BF16)
+        nc.sync.dma_start(out=w_sb[:], in_=weight)
+
+        e_tiles = {}
+
+        def load(t):
+            e_t = epool.tile([P, N], BF16, name="e_t")
+            nc.sync.dma_start(out=e_t[:], in_=edge_index[t * P : (t + 1) * P, :])
+            e_tiles[t] = e_t
+
+        load(0)
+        load(1)
+        bias_bc = const.tile([P, C], BF16)
+        nc.sync.dma_start(out=bias_bc[:], in_=bias.partition_broadcast(P))
+        d_bf = const.tile([P, NT], BF16)
+        with nc.allow_non_contiguous_dma(reason="the 4096 diagonal elements, one each"):
+            nc.sync.dma_start(
+                out=d_bf[:],
+                in_=edge_index.rearrange("a b -> (a b)")[0 : N * N : N + 1].rearrange("(t p) -> p t", p=P),
+            )
+
+        xt_sb = const.tile([P, N], BF16)
+        xg = const.tile([P, N], BF16, align_bytes=64)
+        xq = const.tile([P, N], BF16, align_bytes=64)
+        for g in range(NG):
+            xtp = tpsum.tile([P, 512], BF16, tag="tp")
+            for t in range(4):
+                b = 4 * g + t
+                nc.tensor.transpose(out=xtp[:, P * t : P * t + P], in_=x_sb[:, P * b : P * b + P], identity=ident_b[:])
+            if g % 2 == 0:
+                nc.vector.tensor_copy(out=xt_sb[:, 512 * g : 512 * g + 512], in_=xtp[:])
+            else:
+                nc.scalar.copy(out=xt_sb[:, 512 * g : 512 * g + 512], in_=xtp[:])
+        for g in range(NG):
+            xwp = tpsum.tile([P, 512], F32, tag="tp")
+            xwp2 = tpsum.tile([P, 512], F32, tag="tp")
+            for dst in (xwp, xwp2):
+                for t in range(4):
+                    b = 4 * g + t
+                    nc.tensor.matmul(out=dst[:, P * t : P * t + P], lhsT=xt_sb[:, P * b : P * b + P], rhs=w_sb[:], start=True, stop=True)
+            nc.vector.tensor_copy(
+                out=xg[:, 512 * g : 512 * g + 512].rearrange("p (c t) -> p c t", t=4),
+                in_=xwp[:].rearrange("p (t c) -> p c t", t=4),
+            )
+            nc.scalar.activation(
+                out=xq[:, 512 * g : 512 * g + 512].rearrange("p (c t) -> p c t", t=4),
+                in_=xwp2[:].rearrange("p (t c) -> p c t", t=4),
+                func=ACT.Square,
+            )
+        xg_c = const.tile([P, N // 4], U32, align_bytes=64)
+        xg_s = const.tile([P, N // 4], U8, align_bytes=64)
+        xq_c = const.tile([P, N // 4], U32, align_bytes=64)
+        xq_s = const.tile([P, N // 4], U8, align_bytes=64)
+        nc.vector.quantize_mx(out=xg_c[:].bitcast(FP8X4), scales=xg_s[:], in_=xg[:])
+        nc.vector.quantize_mx(out=xq_c[:].bitcast(FP8X4), scales=xq_s[:], in_=xq[:])
+
+        d32 = const.tile([P, NT], F32)
+        nc.vector.tensor_copy(out=d32[:], in_=d_bf[:])
+        a1 = const.tile([P, NT], F32)
+        nc.vector.tensor_scalar_add(out=a1[:], in0=d32[:], scalar1=1.0)
+        a1b = const.tile([P, NT], BF16)
+        nc.vector.tensor_copy(out=a1b[:], in_=a1[:])
+        resid = const.tile([P, NT], F32)
+        nc.vector.tensor_tensor(out=resid[:], in0=a1[:], in1=a1b[:], op=ALU.subtract)
+        css = const.tile([P, NT], F32)
+        nc.vector.tensor_scalar(out=css[:], in0=d32[:], scalar1=2.0, scalar2=1.0, op0=ALU.mult, op1=ALU.add)
+
+        ss_raw = const.tile([P, NT], F32)
+        junk = const.tile([P, N], BF16)
+        tt = const.tile([P, NT * C], F32)
+        ot = const.tile([P, NT * C], F32)
+        rsp = apsum.tile([P, P], F32)
+        acc = {}
+        grouped = {}
+        codes = {}
+
+        def natural(t):
+            nc.scalar.activation(out=junk[:], in_=e_tiles[t][:], func=ACT.Square, accum_out=ss_raw[:, t : t + 1])
+
+        def transposes(t):
+            gs = t // 4
+            ew = e_tiles[t][:].bitcast(F32)
+            ag = gpool.tile([P, N], BF16, name="ag", align_bytes=64)
+            sg = gpool.tile([P, N], BF16, name="sg", align_bytes=64)
+            grouped[t] = (ag, sg)
+            agw = ag[:].bitcast(F32)
+            for h in range(4):
+                tp = tpsum.tile([P, 512], F32, tag="tp")
+                for k in range(4):
+                    w0 = 512 * h + P * k
+                    nc.tensor.transpose(out=tp[:, P * k : P * k + P], in_=ew[:, w0 : w0 + P], identity=ident_f[:])
+                if gs // 2 != h:
+                    nc.scalar.copy(
+                        out=agw[:, 512 * h : 512 * h + 512].rearrange("p (g i u) -> p g i u", g=2, i=P, u=2),
+                        in_=tp[:].rearrange("p (g u i) -> p g i u", g=2, u=2, i=P),
+                    )
+                else:
+                    g2 = gs % 2
+                    go = 1 - g2
+                    nc.vector.tensor_copy(
+                        out=agw[:, 512 * h + 256 * go : 512 * h + 256 * go + 256].rearrange("p (i u) -> p i u", i=P, u=2),
+                        in_=tp[:, 256 * go : 256 * go + 256].rearrange("p (u i) -> p i u", u=2, i=P),
+                    )
+                    atmp = work.tile([P, 512], F32, name="atmp")
+                    nc.vector.tensor_tensor(
+                        out=atmp[:].rearrange("p (i u e) -> p i u e", i=P, u=2, e=2),
+                        in0=tp[:].bitcast(BF16)[:, 512 * g2 : 512 * g2 + 512].rearrange("p (u i e) -> p i u e", u=2, i=P, e=2),
+                        in1=mask[:, t % 4, :].rearrange("p (i u e) -> p i u e", i=P, u=2, e=2),
+                        op=ALU.add,
+                    )
+                    nc.vector.tensor_copy(out=ag[:, 512 * gs : 512 * gs + 512], in_=atmp[:])
+                    nc.vector.tensor_tensor(out=sg[:, 512 * gs : 512 * gs + 512], in0=atmp[:], in1=atmp[:], op=ALU.mult)
+
+        def squares(t):
+            gs = t // 4
+            ag, sg = grouped[t]
+            for lo, hi in ((0, 512 * gs), (512 * gs + 512, N)):
+                if hi > lo:
+                    nc.vector.tensor_tensor(out=sg[:, lo:hi], in0=ag[:, lo:hi], in1=ag[:, lo:hi], op=ALU.mult)
+
+        def quantise(t):
+            ag, sg = grouped[t]
+            a_c = cpool.tile([P, N // 4], U32, name="a_c", align_bytes=64)
+            a_s = cpool.tile([P, N // 4], U8, name="a_s", align_bytes=64)
+            s_c = cpool.tile([P, N // 4], U32, name="s_c", align_bytes=64)
+            s_s = cpool.tile([P, N // 4], U8, name="s_s", align_bytes=64)
+            nc.vector.quantize_mx(out=a_c[:].bitcast(FP8X4), scales=a_s[:], in_=ag[:])
+            nc.vector.quantize_mx(out=s_c[:].bitcast(FP8X4), scales=s_s[:], in_=sg[:])
+            codes[t] = (a_c, a_s, s_c, s_s)
+
+        def rowsum(t):
+            ag = grouped[t][0]
+            for sub in range(4):
+                col = 4 * t + sub
+                for g in range(NG):
+                    c0 = 512 * g + P * sub
+                    nc.tensor.matmul(out=rsp[:, col : col + 1], lhsT=ag[:, c0 : c0 + P], rhs=ones_b[:, 0:1], start=(g == 0), stop=(g == NG - 1))
+
+        def mx(t):
+            a_c, a_s, s_c, s_s = codes[t]
+            slot = t % 4
+            if slot == 0:
+                sps = apsum.tile([P, 512], F32, name="sps")
+                qps = apsum.tile([P, 512], F32, name="qps")
+                acc[t // 4] = (sps, qps)
+            sps, qps = acc[t // 4]
+            for dst, l_c, l_s, r_c, r_s in ((sps, a_c, a_s, xg_c, xg_s), (qps, s_c, s_s, xq_c, xq_s)):
+                for g in range(NG):
+                    cs = slice(P * g, P * g + P)
+                    nc.tensor.matmul_mx(
+                        out=dst[:, P * slot : P * slot + P],
+                        lhsT=l_c[:, cs].bitcast(FP8X4),
+                        lhsT_scale=l_s[:, cs],
+                        rhs=r_c[:, cs].bitcast(FP8X4),
+                        rhs_scale=r_s[:, cs],
+                        start=(g == 0),
+                        stop=(g == NG - 1),
+                    )
+            if slot == 3:
+                b = t // 4
+                s2 = work.tile([P, 512], F32, name="s2")
+                nc.scalar.activation(out=s2[:], in_=sps[:], func=ACT.Square)
+                nc.vector.tensor_tensor(out=tt[:, 512 * b : 512 * b + 512], in0=s2[:], in1=qps[:], op=ALU.subtract)
+
+        for t in range(NT + 1):
+            if t + 2 < NT:
+                load(t + 2)
+            if t < NT:
+                natural(t)
+                transposes(t)
+            if t >= 1:
+                rowsum(t - 1)
+                mx(t - 1)
+            if t < NT:
+                squares(t)
+                quantise(t)
+
+        r_sb = const.tile([P, P], F32)
+        nc.vector.tensor_copy(out=r_sb[:], in_=rsp[:])
+        rso = tpsum.tile([P, NT], F32, tag="tp")
+        for sub in range(4):
+            nc.tensor.matmul(
+                out=rso[:],
+                lhsT=fold[:, sub, :],
+                rhs=r_sb[:].rearrange("p (t s) -> p s t", s=4)[:, sub, :],
+                start=(sub == 0),
+                stop=(sub == 3),
+            )
+        rs = const.tile([P, NT], F32)
+        nc.vector.tensor_tensor(out=rs[:], in0=rso[:], in1=resid[:], op=ALU.add)
+        ssa = const.tile([P, NT], F32)
+        nc.vector.tensor_tensor(out=ssa[:], in0=ss_raw[:], in1=css[:], op=ALU.add)
+        r2 = const.tile([P, NT], F32)
+        nc.vector.tensor_tensor(out=r2[:], in0=rs[:], in1=rs[:], op=ALU.mult)
+        den = const.tile([P, NT], F32)
+        nc.vector.tensor_tensor(out=den[:], in0=r2[:], in1=ssa[:], op=ALU.subtract)
+        nz = const.tile([P, NT], F32)
+        nc.vector.tensor_single_scalar(out=nz[:], in_=den[:], scalar=0.0, op=ALU.not_equal)
+        pad = const.tile([P, NT], F32)
+        nc.vector.tensor_scalar(out=pad[:], in0=nz[:], scalar1=-1.0, scalar2=1.0, op0=ALU.mult, op1=ALU.add)
+        dsafe = const.tile([P, NT], F32)
+        nc.vector.tensor_tensor(out=dsafe[:], in0=den[:], in1=pad[:], op=ALU.add)
+        rec = const.tile([P, NT], F32)
+        nc.vector.reciprocal(out=rec[:], in_=dsafe[:])
+        norm = const.tile([P, NT], F32)
+        nc.vector.tensor_tensor(out=norm[:], in0=rec[:], in1=nz[:], op=ALU.mult)
+
+        out_v = out.rearrange("(t p) c -> p t c", p=P)
+        for t in range(NT):
+            nc.vector.scalar_tensor_tensor(
+                out=ot[:, C * t : C * t + C],
+                in0=tt[:, C * t : C * t + C],
+                scalar=norm[:, t : t + 1],
+                in1=bias_bc[:],
+                op0=ALU.mult,
+                op1=ALU.add,
+            )
+            if t % 8 == 7:
+                k = t // 8
+                nc.sync.dma_start(
+                    out=out_v[:, 8 * k : 8 * k + 8, :],
+                    in_=ot[:, 1024 * k : 1024 * k + 1024].rearrange("p (t c) -> p t c", c=C),
+                )

@@ -19,47 +19,23 @@ NT = N // P
 NG = N // 512
 FLOPS = 2 * N * N * C * 2 + 2 * N * C * C
 
+PIN = True
+SEG_CAST = "V"
+SEG_SQ = "S"
+
 
 def tile_bgnna_kernel(tc, x, edge_index, weight, bias, out):
     nc = tc.nc
     with ExitStack() as ctx:
         const = ctx.enter_context(tc.tile_pool(name="const", bufs=1))
         epool = ctx.enter_context(tc.tile_pool(name="epool", bufs=4))
-        gpool = ctx.enter_context(tc.tile_pool(name="gpool", bufs=2))
-        cpool = ctx.enter_context(tc.tile_pool(name="cpool", bufs=2))
+        gpool = ctx.enter_context(tc.tile_pool(name="gpool", bufs=3))
+        cpool = ctx.enter_context(tc.tile_pool(name="cpool", bufs=3))
         work = ctx.enter_context(tc.tile_pool(name="work", bufs=2))
-        tpsum = ctx.enter_context(tc.psum_pool(name="tpsum", bufs=4))
+        tpsum = ctx.enter_context(tc.psum_pool(name="tpsum", bufs=5))
         apsum = ctx.enter_context(tc.psum_pool(name="apsum", bufs=1))
-
-        ident_f = const.tile([P, P], F32)
-        make_identity(nc, ident_f[:])
-        ident_b = const.tile([P, P], BF16)
-        make_identity(nc, ident_b[:])
-        ones_b = const.tile([P, 2], BF16)
-        nc.vector.memset(ones_b[:], 1.0)
-
-        mask = const.tile([P, 4, 512], BF16)
-        nc.vector.memset(mask[:], 0.0)
-        for v in range(4):
-            u_t, par = v // 2, v % 2
-            mv = mask[:, v, :].rearrange("p (h e t) -> p h e t", h=64, e=2, t=4)
-            for e in range(2):
-                nc.vector.tensor_copy(out=mv[:, :, e, 2 * u_t + e], in_=ident_b[:, 64 * par : 64 * par + 64])
-
-        gsel = const.tile([P, 32], F32)
-        nc.vector.tensor_reduce(out=gsel[:], in_=ident_f[:].rearrange("p (c t) -> p c t", t=4), axis=AX.X, op=ALU.add)
-        fold = const.tile([P, 4, P], F32)
-        nc.vector.memset(fold[:], 0.0)
-        for sub in range(4):
-            nc.vector.tensor_copy(out=fold[:, sub, 32 * sub : 32 * sub + 32], in_=gsel[:])
-
-        x_sb = const.tile([P, N], BF16)
-        nc.sync.dma_start(
-            out=x_sb[:].rearrange("q (a r) -> q a r", a=16),
-            in_=x.rearrange("(a q e) i -> q a (e i)", a=16, q=P, e=2),
-        )
-        w_sb = const.tile([P, C], BF16)
-        nc.sync.dma_start(out=w_sb[:], in_=weight)
+        if PIN:
+            ctx.enter_context(tc.manual_schedule())
 
         e_tiles = {}
 
@@ -69,7 +45,15 @@ def tile_bgnna_kernel(tc, x, edge_index, weight, bias, out):
             e_tiles[t] = e_t
 
         load(0)
+        x_sb = const.tile([P, N], BF16)
+        nc.sync.dma_start(
+            out=x_sb[:].rearrange("q (a r) -> q a r", a=16),
+            in_=x.rearrange("(a q e) i -> q a (e i)", a=16, q=P, e=2),
+        )
+        w_sb = const.tile([P, C], BF16)
+        nc.sync.dma_start(out=w_sb[:], in_=weight)
         load(1)
+        load(2)
         bias_bc = const.tile([P, C], BF16)
         nc.sync.dma_start(out=bias_bc[:], in_=bias.partition_broadcast(P))
         d_bf = const.tile([P, NT], BF16)
@@ -79,51 +63,25 @@ def tile_bgnna_kernel(tc, x, edge_index, weight, bias, out):
                 in_=edge_index.rearrange("a b -> (a b)")[0 : N * N : N + 1].rearrange("(t p) -> p t", p=P),
             )
 
-        xt_sb = const.tile([P, N], BF16)
-        xg = const.tile([P, N], BF16, align_bytes=64)
-        xq = const.tile([P, N], BF16, align_bytes=64)
-        for g in range(NG):
-            xtp = tpsum.tile([P, 512], BF16, tag="tp")
-            for t in range(4):
-                b = 4 * g + t
-                nc.tensor.transpose(out=xtp[:, P * t : P * t + P], in_=x_sb[:, P * b : P * b + P], identity=ident_b[:])
-            if g % 2 == 0:
-                nc.vector.tensor_copy(out=xt_sb[:, 512 * g : 512 * g + 512], in_=xtp[:])
-            else:
-                nc.scalar.copy(out=xt_sb[:, 512 * g : 512 * g + 512], in_=xtp[:])
-        for g in range(NG):
-            xwp = tpsum.tile([P, 512], F32, tag="tp")
-            xwp2 = tpsum.tile([P, 512], F32, tag="tp")
-            for dst in (xwp, xwp2):
-                for t in range(4):
-                    b = 4 * g + t
-                    nc.tensor.matmul(out=dst[:, P * t : P * t + P], lhsT=xt_sb[:, P * b : P * b + P], rhs=w_sb[:], start=True, stop=True)
-            nc.vector.tensor_copy(
-                out=xg[:, 512 * g : 512 * g + 512].rearrange("p (c t) -> p c t", t=4),
-                in_=xwp[:].rearrange("p (t c) -> p c t", t=4),
-            )
-            nc.scalar.activation(
-                out=xq[:, 512 * g : 512 * g + 512].rearrange("p (c t) -> p c t", t=4),
-                in_=xwp2[:].rearrange("p (t c) -> p c t", t=4),
-                func=ACT.Square,
-            )
-        xg_c = const.tile([P, N // 4], U32, align_bytes=64)
-        xg_s = const.tile([P, N // 4], U8, align_bytes=64)
-        xq_c = const.tile([P, N // 4], U32, align_bytes=64)
-        xq_s = const.tile([P, N // 4], U8, align_bytes=64)
-        nc.vector.quantize_mx(out=xg_c[:].bitcast(FP8X4), scales=xg_s[:], in_=xg[:])
-        nc.vector.quantize_mx(out=xq_c[:].bitcast(FP8X4), scales=xq_s[:], in_=xq[:])
-
-        d32 = const.tile([P, NT], F32)
-        nc.vector.tensor_copy(out=d32[:], in_=d_bf[:])
-        a1 = const.tile([P, NT], F32)
-        nc.vector.tensor_scalar_add(out=a1[:], in0=d32[:], scalar1=1.0)
-        a1b = const.tile([P, NT], BF16)
-        nc.vector.tensor_copy(out=a1b[:], in_=a1[:])
-        resid = const.tile([P, NT], F32)
-        nc.vector.tensor_tensor(out=resid[:], in0=a1[:], in1=a1b[:], op=ALU.subtract)
-        css = const.tile([P, NT], F32)
-        nc.vector.tensor_scalar(out=css[:], in0=d32[:], scalar1=2.0, scalar2=1.0, op0=ALU.mult, op1=ALU.add)
+        ident_f = const.tile([P, P], F32)
+        make_identity(nc, ident_f[:])
+        ident_b = const.tile([P, P], BF16)
+        nc.vector.tensor_copy(out=ident_b[:], in_=ident_f[:])
+        ones_b = const.tile([P, 2], BF16)
+        nc.vector.memset(ones_b[:], 1.0)
+        mask = const.tile([P, 4, 512], BF16)
+        nc.vector.memset(mask[:], 0.0)
+        for v in range(4):
+            u_t, par = v // 2, v % 2
+            mv = mask[:, v, :].rearrange("p (h e t) -> p h e t", h=64, e=2, t=4)
+            for e in range(2):
+                nc.vector.tensor_copy(out=mv[:, :, e, 2 * u_t + e], in_=ident_b[:, 64 * par : 64 * par + 64])
+        gsel = const.tile([P, 32], F32)
+        nc.vector.tensor_reduce(out=gsel[:], in_=ident_f[:].rearrange("p (c t) -> p c t", t=4), axis=AX.X, op=ALU.add)
+        fold = const.tile([P, 4, P], F32)
+        nc.vector.memset(fold[:], 0.0)
+        for sub in range(4):
+            nc.vector.tensor_copy(out=fold[:, sub, 32 * sub : 32 * sub + 32], in_=gsel[:])
 
         ss_raw = const.tile([P, NT], F32)
         junk = const.tile([P, N], BF16)
@@ -133,43 +91,85 @@ def tile_bgnna_kernel(tc, x, edge_index, weight, bias, out):
         acc = {}
         grouped = {}
         codes = {}
+        banks = {}
+        atmps = {}
 
         def natural(t):
             nc.scalar.activation(out=junk[:], in_=e_tiles[t][:], func=ACT.Square, accum_out=ss_raw[:, t : t + 1])
 
+        def bank_order(t):
+            hs = (t // 4) // 2
+            return [hs] + [h for h in range(4) if h != hs]
+
         def transposes(t):
-            gs = t // 4
             ew = e_tiles[t][:].bitcast(F32)
-            ag = gpool.tile([P, N], BF16, name="ag", align_bytes=64)
-            sg = gpool.tile([P, N], BF16, name="sg", align_bytes=64)
-            grouped[t] = (ag, sg)
-            agw = ag[:].bitcast(F32)
-            for h in range(4):
+            for h in bank_order(t):
                 tp = tpsum.tile([P, 512], F32, tag="tp")
                 for k in range(4):
                     w0 = 512 * h + P * k
                     nc.tensor.transpose(out=tp[:, P * k : P * k + P], in_=ew[:, w0 : w0 + P], identity=ident_f[:])
-                if gs // 2 != h:
-                    nc.scalar.copy(
-                        out=agw[:, 512 * h : 512 * h + 512].rearrange("p (g i u) -> p g i u", g=2, i=P, u=2),
-                        in_=tp[:].rearrange("p (g u i) -> p g i u", g=2, u=2, i=P),
-                    )
-                else:
-                    g2 = gs % 2
-                    go = 1 - g2
-                    nc.vector.tensor_copy(
-                        out=agw[:, 512 * h + 256 * go : 512 * h + 256 * go + 256].rearrange("p (i u) -> p i u", i=P, u=2),
-                        in_=tp[:, 256 * go : 256 * go + 256].rearrange("p (u i) -> p i u", u=2, i=P),
-                    )
-                    atmp = work.tile([P, 512], F32, name="atmp")
-                    nc.vector.tensor_tensor(
-                        out=atmp[:].rearrange("p (i u e) -> p i u e", i=P, u=2, e=2),
-                        in0=tp[:].bitcast(BF16)[:, 512 * g2 : 512 * g2 + 512].rearrange("p (u i e) -> p i u e", u=2, i=P, e=2),
-                        in1=mask[:, t % 4, :].rearrange("p (i u e) -> p i u e", i=P, u=2, e=2),
-                        op=ALU.add,
-                    )
-                    nc.vector.tensor_copy(out=ag[:, 512 * gs : 512 * gs + 512], in_=atmp[:])
-                    nc.vector.tensor_tensor(out=sg[:, 512 * gs : 512 * gs + 512], in0=atmp[:], in1=atmp[:], op=ALU.mult)
+                banks[(t, h)] = tp
+
+        def alloc_grouped(t):
+            ag = gpool.tile([P, N], BF16, name="ag", align_bytes=64)
+            sg = gpool.tile([P, N], BF16, name="sg", align_bytes=64)
+            grouped[t] = (ag, sg)
+
+        def special_a(t):
+            gs = t // 4
+            h = gs // 2
+            g2 = gs % 2
+            go = 1 - g2
+            tp = banks[(t, h)]
+            agw = grouped[t][0][:].bitcast(F32)
+            atmp = work.tile([P, 512], F32, name="atmp")
+            atmps[t] = atmp
+            nc.vector.tensor_tensor(
+                out=atmp[:].rearrange("p (i u e) -> p i u e", i=P, u=2, e=2),
+                in0=tp[:].bitcast(BF16)[:, 512 * g2 : 512 * g2 + 512].rearrange("p (u i e) -> p i u e", u=2, i=P, e=2),
+                in1=mask[:, t % 4, :].rearrange("p (i u e) -> p i u e", i=P, u=2, e=2),
+                op=ALU.add,
+            )
+            nc.vector.tensor_copy(
+                out=agw[:, 512 * h + 256 * go : 512 * h + 256 * go + 256].rearrange("p (i u) -> p i u", i=P, u=2),
+                in_=tp[:, 256 * go : 256 * go + 256].rearrange("p (u i) -> p i u", u=2, i=P),
+            )
+
+        def special_cast(t):
+            gs = t // 4
+            ag = grouped[t][0]
+            dst = ag[:, 512 * gs : 512 * gs + 512]
+            if SEG_CAST == "V":
+                nc.vector.tensor_copy(out=dst, in_=atmps[t][:])
+            elif SEG_CAST == "S":
+                nc.scalar.copy(out=dst, in_=atmps[t][:])
+            else:
+                nc.gpsimd.tensor_scalar(out=dst, in0=atmps[t][:], scalar1=1.0, scalar2=0.0, op0=ALU.mult, op1=ALU.add)
+
+        def special_sq(t):
+            gs = t // 4
+            sg = grouped[t][1]
+            dst = sg[:, 512 * gs : 512 * gs + 512]
+            if SEG_SQ == "V":
+                nc.vector.tensor_tensor(out=dst, in0=atmps[t][:], in1=atmps[t][:], op=ALU.mult)
+            elif SEG_SQ == "S":
+                nc.scalar.activation(out=dst, in_=atmps[t][:], func=ACT.Square)
+            else:
+                nc.gpsimd.tensor_tensor(out=dst, in0=atmps[t][:], in1=atmps[t][:], op=ALU.mult)
+
+        def copy_bank(t, h, eng):
+            agw = grouped[t][0][:].bitcast(F32)
+            dst = agw[:, 512 * h : 512 * h + 512].rearrange("p (g i u) -> p g i u", g=2, i=P, u=2)
+            src = banks[(t, h)][:].rearrange("p (g u i) -> p g i u", g=2, u=2, i=P)
+            if eng == "S":
+                nc.scalar.copy(out=dst, in_=src)
+            else:
+                nc.vector.tensor_copy(out=dst, in_=src)
+
+        def v_banks(t):
+            if t == 0:
+                return 3
+            return 1 if t % 3 != 0 else 0
 
         def squares(t):
             gs = t // 4
@@ -178,15 +178,20 @@ def tile_bgnna_kernel(tc, x, edge_index, weight, bias, out):
                 if hi > lo:
                     nc.vector.tensor_tensor(out=sg[:, lo:hi], in0=ag[:, lo:hi], in1=ag[:, lo:hi], op=ALU.mult)
 
-        def quantise(t):
-            ag, sg = grouped[t]
+        def alloc_codes(t):
             a_c = cpool.tile([P, N // 4], U32, name="a_c", align_bytes=64)
             a_s = cpool.tile([P, N // 4], U8, name="a_s", align_bytes=64)
             s_c = cpool.tile([P, N // 4], U32, name="s_c", align_bytes=64)
             s_s = cpool.tile([P, N // 4], U8, name="s_s", align_bytes=64)
-            nc.vector.quantize_mx(out=a_c[:].bitcast(FP8X4), scales=a_s[:], in_=ag[:])
-            nc.vector.quantize_mx(out=s_c[:].bitcast(FP8X4), scales=s_s[:], in_=sg[:])
             codes[t] = (a_c, a_s, s_c, s_s)
+
+        def quant_a(t):
+            a_c, a_s = codes[t][0], codes[t][1]
+            nc.vector.quantize_mx(out=a_c[:].bitcast(FP8X4), scales=a_s[:], in_=grouped[t][0][:])
+
+        def quant_s(t):
+            s_c, s_s = codes[t][2], codes[t][3]
+            nc.vector.quantize_mx(out=s_c[:].bitcast(FP8X4), scales=s_s[:], in_=grouped[t][1][:])
 
         def rowsum(t):
             ag = grouped[t][0]
@@ -196,8 +201,11 @@ def tile_bgnna_kernel(tc, x, edge_index, weight, bias, out):
                     c0 = 512 * g + P * sub
                     nc.tensor.matmul(out=rsp[:, col : col + 1], lhsT=ag[:, c0 : c0 + P], rhs=ones_b[:, 0:1], start=(g == 0), stop=(g == NG - 1))
 
+        xw = {}
+
         def mx(t):
             a_c, a_s, s_c, s_s = codes[t]
+            xg_c, xg_s, xq_c, xq_s = xw["codes"]
             slot = t % 4
             if slot == 0:
                 sps = apsum.tile([P, 512], F32, name="sps")
@@ -216,57 +224,144 @@ def tile_bgnna_kernel(tc, x, edge_index, weight, bias, out):
                         start=(g == 0),
                         stop=(g == NG - 1),
                     )
-            if slot == 3:
-                b = t // 4
-                s2 = work.tile([P, 512], F32, name="s2")
-                nc.scalar.activation(out=s2[:], in_=sps[:], func=ACT.Square)
-                nc.vector.tensor_tensor(out=tt[:, 512 * b : 512 * b + 512], in0=s2[:], in1=qps[:], op=ALU.subtract)
 
-        for t in range(NT + 1):
-            if t + 2 < NT:
-                load(t + 2)
-            if t < NT:
-                natural(t)
-                transposes(t)
-            if t >= 1:
-                rowsum(t - 1)
-                mx(t - 1)
-            if t < NT:
-                squares(t)
-                quantise(t)
+        s2s = {}
+
+        def epi_s(b):
+            s2 = work.tile([P, 512], F32, name="s2")
+            s2s[b] = s2
+            nc.scalar.activation(out=s2[:], in_=acc[b][0][:], func=ACT.Square)
+
+        def epi_v(b):
+            nc.vector.tensor_tensor(out=tt[:, 512 * b : 512 * b + 512], in0=s2s[b][:], in1=acc[b][1][:], op=ALU.subtract)
+
+        natural(0)
+        transposes(0)
+        alloc_grouped(0)
+        special_a(0)
+        for h in bank_order(0)[1:]:
+            copy_bank(0, h, "V")
+        special_cast(0)
+        special_sq(0)
+
+        xt_sb = const.tile([P, N], BF16)
+        xg = const.tile([P, N], BF16, align_bytes=64)
+        xq = const.tile([P, N], BF16, align_bytes=64)
+        for g2 in range(NG // 2):
+            xtp = tpsum.tile([P, 1024], BF16, tag="tp")
+            for t in range(8):
+                b = 8 * g2 + t
+                nc.tensor.transpose(out=xtp[:, P * t : P * t + P], in_=x_sb[:, P * b : P * b + P], identity=ident_b[:])
+            nc.scalar.copy(out=xt_sb[:, 1024 * g2 : 1024 * g2 + 1024], in_=xtp[:])
+
+        def xw_stage():
+            for g in range(NG):
+                xwp = tpsum.tile([P, 512], F32, tag="tp")
+                xwp2 = tpsum.tile([P, 512], F32, tag="tp")
+                for dst in (xwp, xwp2):
+                    for t in range(4):
+                        b = 4 * g + t
+                        nc.tensor.matmul(out=dst[:, P * t : P * t + P], lhsT=xt_sb[:, P * b : P * b + P], rhs=w_sb[:], start=True, stop=True)
+                nc.vector.tensor_copy(
+                    out=xg[:, 512 * g : 512 * g + 512].rearrange("p (c t) -> p c t", t=4),
+                    in_=xwp[:].rearrange("p (t c) -> p c t", t=4),
+                )
+                nc.scalar.activation(
+                    out=xq[:, 512 * g : 512 * g + 512].rearrange("p (c t) -> p c t", t=4),
+                    in_=xwp2[:].rearrange("p (t c) -> p c t", t=4),
+                    func=ACT.Square,
+                )
+            xg_c = const.tile([P, N // 4], U32, align_bytes=64)
+            xg_s = const.tile([P, N // 4], U8, align_bytes=64)
+            xq_c = const.tile([P, N // 4], U32, align_bytes=64)
+            xq_s = const.tile([P, N // 4], U8, align_bytes=64)
+            xw["codes"] = (xg_c, xg_s, xq_c, xq_s)
+            nc.vector.quantize_mx(out=xg_c[:].bitcast(FP8X4), scales=xg_s[:], in_=xg[:])
+            nc.vector.quantize_mx(out=xq_c[:].bitcast(FP8X4), scales=xq_s[:], in_=xq[:])
+
+        d32 = const.tile([P, NT], F32)
+        a1 = const.tile([P, NT], F32)
+        a1b = const.tile([P, NT], BF16)
+        resid = const.tile([P, NT], F32)
+        css = const.tile([P, NT], F32)
+
+        def diag_scalars():
+            nc.vector.tensor_copy(out=d32[:], in_=d_bf[:])
+            nc.vector.tensor_scalar_add(out=a1[:], in0=d32[:], scalar1=1.0)
+            nc.vector.tensor_copy(out=a1b[:], in_=a1[:])
+            nc.vector.tensor_tensor(out=resid[:], in0=a1[:], in1=a1b[:], op=ALU.subtract)
+            nc.vector.tensor_scalar(out=css[:], in0=d32[:], scalar1=2.0, scalar2=1.0, op0=ALU.mult, op1=ALU.add)
 
         r_sb = const.tile([P, P], F32)
-        nc.vector.tensor_copy(out=r_sb[:], in_=rsp[:])
-        rso = tpsum.tile([P, NT], F32, tag="tp")
-        for sub in range(4):
-            nc.tensor.matmul(
-                out=rso[:],
-                lhsT=fold[:, sub, :],
-                rhs=r_sb[:].rearrange("p (t s) -> p s t", s=4)[:, sub, :],
-                start=(sub == 0),
-                stop=(sub == 3),
-            )
         rs = const.tile([P, NT], F32)
-        nc.vector.tensor_tensor(out=rs[:], in0=rso[:], in1=resid[:], op=ALU.add)
         ssa = const.tile([P, NT], F32)
-        nc.vector.tensor_tensor(out=ssa[:], in0=ss_raw[:], in1=css[:], op=ALU.add)
         r2 = const.tile([P, NT], F32)
-        nc.vector.tensor_tensor(out=r2[:], in0=rs[:], in1=rs[:], op=ALU.mult)
         den = const.tile([P, NT], F32)
-        nc.vector.tensor_tensor(out=den[:], in0=r2[:], in1=ssa[:], op=ALU.subtract)
         nz = const.tile([P, NT], F32)
-        nc.vector.tensor_single_scalar(out=nz[:], in_=den[:], scalar=0.0, op=ALU.not_equal)
         pad = const.tile([P, NT], F32)
-        nc.vector.tensor_scalar(out=pad[:], in0=nz[:], scalar1=-1.0, scalar2=1.0, op0=ALU.mult, op1=ALU.add)
         dsafe = const.tile([P, NT], F32)
-        nc.vector.tensor_tensor(out=dsafe[:], in0=den[:], in1=pad[:], op=ALU.add)
         rec = const.tile([P, NT], F32)
-        nc.vector.reciprocal(out=rec[:], in_=dsafe[:])
         norm = const.tile([P, NT], F32)
+
+        load(3)
+        for i in range(NT):
+            if i == 1:
+                xw_stage()
+                diag_scalars()
+            if i + 1 < NT:
+                transposes(i + 1)
+            if i >= 1:
+                mx(i - 1)
+                if (i - 1) % 4 == 3:
+                    epi_s((i - 1) // 4)
+            rowsum(i)
+            squares(i)
+            if i + 1 < NT:
+                alloc_grouped(i + 1)
+                special_a(i + 1)
+                nv = v_banks(i + 1)
+                reg = bank_order(i + 1)[1:]
+                for j, h in enumerate(reg):
+                    copy_bank(i + 1, h, "V" if j < nv else "S")
+            else:
+                nc.vector.tensor_copy(out=r_sb[:], in_=rsp[:])
+                rso = tpsum.tile([P, NT], F32, tag="tp")
+                for sub in range(4):
+                    nc.tensor.matmul(
+                        out=rso[:],
+                        lhsT=fold[:, sub, :],
+                        rhs=r_sb[:].rearrange("p (t s) -> p s t", s=4)[:, sub, :],
+                        start=(sub == 0),
+                        stop=(sub == 3),
+                    )
+            alloc_codes(i)
+            quant_a(i)
+            if i + 1 < NT:
+                special_cast(i + 1)
+                natural(i + 1)
+                special_sq(i + 1)
+            quant_s(i)
+            if i >= 1 and (i - 1) % 4 == 3:
+                epi_v((i - 1) // 4)
+            if i + 4 < NT:
+                load(i + 4)
+        mx(NT - 1)
+        epi_s(NT // 4 - 1)
+
+        nc.vector.tensor_tensor(out=rs[:], in0=rso[:], in1=resid[:], op=ALU.add)
+        nc.vector.tensor_tensor(out=ssa[:], in0=ss_raw[:], in1=css[:], op=ALU.add)
+        nc.vector.tensor_tensor(out=r2[:], in0=rs[:], in1=rs[:], op=ALU.mult)
+        nc.vector.tensor_tensor(out=den[:], in0=r2[:], in1=ssa[:], op=ALU.subtract)
+        nc.vector.tensor_single_scalar(out=nz[:], in_=den[:], scalar=0.0, op=ALU.not_equal)
+        nc.vector.tensor_scalar(out=pad[:], in0=nz[:], scalar1=-1.0, scalar2=1.0, op0=ALU.mult, op1=ALU.add)
+        nc.vector.tensor_tensor(out=dsafe[:], in0=den[:], in1=pad[:], op=ALU.add)
+        nc.vector.reciprocal(out=rec[:], in_=dsafe[:])
         nc.vector.tensor_tensor(out=norm[:], in0=rec[:], in1=nz[:], op=ALU.mult)
 
         out_v = out.rearrange("(t p) c -> p t c", p=P)
         for t in range(NT):
+            if t == NT - 4:
+                epi_v(NT // 4 - 1)
             nc.vector.scalar_tensor_tensor(
                 out=ot[:, C * t : C * t + C],
                 in0=tt[:, C * t : C * t + C],
@@ -275,9 +370,9 @@ def tile_bgnna_kernel(tc, x, edge_index, weight, bias, out):
                 op0=ALU.mult,
                 op1=ALU.add,
             )
-            if t % 8 == 7:
-                k = t // 8
+            if t % 8 == 7 or t == NT - 5:
+                lo = 8 * (t // 8) if t % 8 == 7 and t != NT - 1 else (NT - 8 if t == NT - 5 else NT - 4)
                 nc.sync.dma_start(
-                    out=out_v[:, 8 * k : 8 * k + 8, :],
-                    in_=ot[:, 1024 * k : 1024 * k + 1024].rearrange("p (t c) -> p t c", c=C),
+                    out=out_v[:, lo : t + 1, :],
+                    in_=ot[:, C * lo : C * (t + 1)].rearrange("p (t c) -> p t c", c=C),
                 )

@@ -20,8 +20,10 @@ NG = N // 512
 FLOPS = 2 * N * N * C * 2 + 2 * N * C * C
 
 PIN = True
-SEG_CAST = "V"
-SEG_SQ = "S"
+GRAM = (3, 11, 19, 27)
+V_BANK_TILES = ()
+SEG_CAST = "G"
+SEG_SQ = "G"
 
 
 def tile_bgnna_kernel(tc, x, edge_index, weight, bias, out):
@@ -44,7 +46,10 @@ def tile_bgnna_kernel(tc, x, edge_index, weight, bias, out):
             nc.sync.dma_start(out=e_t[:], in_=edge_index[t * P : (t + 1) * P, :])
             e_tiles[t] = e_t
 
-        load(0)
+        e_0 = epool.tile([P, N], BF16, name="e_t")
+        e_tiles[0] = e_0
+        for h in range(4):
+            nc.sync.dma_start(out=e_0[:, 1024 * h : 1024 * h + 1024], in_=edge_index[0:P, 1024 * h : 1024 * h + 1024])
         x_sb = const.tile([P, N], BF16)
         nc.sync.dma_start(
             out=x_sb[:].rearrange("q (a r) -> q a r", a=16),
@@ -84,6 +89,10 @@ def tile_bgnna_kernel(tc, x, edge_index, weight, bias, out):
             nc.vector.tensor_copy(out=fold[:, sub, 32 * sub : 32 * sub + 32], in_=gsel[:])
 
         ss_raw = const.tile([P, NT], F32)
+        nc.vector.memset(ss_raw[:], 0.0)
+        ss_0 = const.tile([P, 4], F32)
+        ssp_sb = const.tile([P, P], F32)
+        nc.vector.memset(ssp_sb[:], 0.0)
         junk = const.tile([P, N], BF16)
         tt = const.tile([P, NT * C], F32)
         ot = const.tile([P, NT * C], F32)
@@ -95,7 +104,34 @@ def tile_bgnna_kernel(tc, x, edge_index, weight, bias, out):
         atmps = {}
 
         def natural(t):
+            if t in GRAM:
+                return
             nc.scalar.activation(out=junk[:], in_=e_tiles[t][:], func=ACT.Square, accum_out=ss_raw[:, t : t + 1])
+
+        grams = {}
+
+        def gram(t):
+            if t not in GRAM:
+                return
+            ag = grouped[t][0]
+            gr = tpsum.tile([P, 512], F32, tag="tp")
+            grams[t] = gr
+            for sub in range(4):
+                for g in range(NG):
+                    c0 = 512 * g + P * sub
+                    nc.tensor.matmul(out=gr[:, P * sub : P * sub + P], lhsT=ag[:, c0 : c0 + P], rhs=ag[:, c0 : c0 + P], start=(g == 0), stop=(g == NG - 1))
+
+        def gram_diag(t):
+            if t not in GRAM:
+                return
+            gtmp = work.tile([P, 512], F32, name="gtmp")
+            nc.vector.tensor_tensor(
+                out=gtmp[:].rearrange("p (s m) -> p s m", s=4),
+                in0=grams[t][:].rearrange("p (s m) -> p s m", s=4),
+                in1=ident_f[:].unsqueeze(1).to_broadcast([P, 4, P]),
+                op=ALU.mult,
+            )
+            nc.vector.tensor_reduce(out=ssp_sb[:, 4 * t : 4 * t + 4], in_=gtmp[:].rearrange("p (s m) -> p s m", s=4), axis=AX.X, op=ALU.add)
 
         def bank_order(t):
             hs = (t // 4) // 2
@@ -169,7 +205,7 @@ def tile_bgnna_kernel(tc, x, edge_index, weight, bias, out):
         def v_banks(t):
             if t == 0:
                 return 3
-            return 1 if t % 3 != 0 else 0
+            return 1 if t % 8 in V_BANK_TILES else 0
 
         def squares(t):
             gs = t // 4
@@ -235,7 +271,8 @@ def tile_bgnna_kernel(tc, x, edge_index, weight, bias, out):
         def epi_v(b):
             nc.vector.tensor_tensor(out=tt[:, 512 * b : 512 * b + 512], in0=s2s[b][:], in1=acc[b][1][:], op=ALU.subtract)
 
-        natural(0)
+        for h in range(4):
+            nc.scalar.activation(out=junk[:, 1024 * h : 1024 * h + 1024], in_=e_0[:, 1024 * h : 1024 * h + 1024], func=ACT.Square, accum_out=ss_0[:, h : h + 1])
         transposes(0)
         alloc_grouped(0)
         special_a(0)
@@ -257,18 +294,16 @@ def tile_bgnna_kernel(tc, x, edge_index, weight, bias, out):
         def xw_stage():
             for g in range(NG):
                 xwp = tpsum.tile([P, 512], F32, tag="tp")
-                xwp2 = tpsum.tile([P, 512], F32, tag="tp")
-                for dst in (xwp, xwp2):
-                    for t in range(4):
-                        b = 4 * g + t
-                        nc.tensor.matmul(out=dst[:, P * t : P * t + P], lhsT=xt_sb[:, P * b : P * b + P], rhs=w_sb[:], start=True, stop=True)
+                for t in range(4):
+                    b = 4 * g + t
+                    nc.tensor.matmul(out=xwp[:, P * t : P * t + P], lhsT=xt_sb[:, P * b : P * b + P], rhs=w_sb[:], start=True, stop=True)
                 nc.vector.tensor_copy(
                     out=xg[:, 512 * g : 512 * g + 512].rearrange("p (c t) -> p c t", t=4),
                     in_=xwp[:].rearrange("p (t c) -> p c t", t=4),
                 )
                 nc.scalar.activation(
                     out=xq[:, 512 * g : 512 * g + 512].rearrange("p (c t) -> p c t", t=4),
-                    in_=xwp2[:].rearrange("p (t c) -> p c t", t=4),
+                    in_=xwp[:].rearrange("p (t c) -> p c t", t=4),
                     func=ACT.Square,
                 )
             xg_c = const.tile([P, N // 4], U32, align_bytes=64)
@@ -284,6 +319,9 @@ def tile_bgnna_kernel(tc, x, edge_index, weight, bias, out):
         a1b = const.tile([P, NT], BF16)
         resid = const.tile([P, NT], F32)
         css = const.tile([P, NT], F32)
+        sq_a = const.tile([P, NT], F32)
+        sq_b = const.tile([P, NT], F32)
+        s0sum = const.tile([P, 1], F32)
 
         def diag_scalars():
             nc.vector.tensor_copy(out=d32[:], in_=d_bf[:])
@@ -291,10 +329,16 @@ def tile_bgnna_kernel(tc, x, edge_index, weight, bias, out):
             nc.vector.tensor_copy(out=a1b[:], in_=a1[:])
             nc.vector.tensor_tensor(out=resid[:], in0=a1[:], in1=a1b[:], op=ALU.subtract)
             nc.vector.tensor_scalar(out=css[:], in0=d32[:], scalar1=2.0, scalar2=1.0, op0=ALU.mult, op1=ALU.add)
+            nc.vector.tensor_tensor(out=sq_a[:], in0=a1[:], in1=a1[:], op=ALU.mult)
+            nc.vector.tensor_tensor(out=sq_b[:], in0=a1b[:], in1=a1b[:], op=ALU.mult)
+            nc.vector.tensor_tensor(out=css[:, GRAM[0] : NT : 8], in0=sq_a[:, GRAM[0] : NT : 8], in1=sq_b[:, GRAM[0] : NT : 8], op=ALU.subtract)
+            nc.vector.tensor_reduce(out=s0sum[:], in_=ss_0[:], axis=AX.X, op=ALU.add)
+            nc.vector.tensor_tensor(out=css[:, 0:1], in0=css[:, 0:1], in1=s0sum[:], op=ALU.add)
 
         r_sb = const.tile([P, P], F32)
         rs = const.tile([P, NT], F32)
         ssa = const.tile([P, NT], F32)
+        ssb = const.tile([P, NT], F32)
         r2 = const.tile([P, NT], F32)
         den = const.tile([P, NT], F32)
         nz = const.tile([P, NT], F32)
@@ -315,6 +359,7 @@ def tile_bgnna_kernel(tc, x, edge_index, weight, bias, out):
                 if (i - 1) % 4 == 3:
                     epi_s((i - 1) // 4)
             rowsum(i)
+            gram(i)
             squares(i)
             if i + 1 < NT:
                 alloc_grouped(i + 1)
@@ -325,15 +370,16 @@ def tile_bgnna_kernel(tc, x, edge_index, weight, bias, out):
                     copy_bank(i + 1, h, "V" if j < nv else "S")
             else:
                 nc.vector.tensor_copy(out=r_sb[:], in_=rsp[:])
-                rso = tpsum.tile([P, NT], F32, tag="tp")
-                for sub in range(4):
-                    nc.tensor.matmul(
-                        out=rso[:],
-                        lhsT=fold[:, sub, :],
-                        rhs=r_sb[:].rearrange("p (t s) -> p s t", s=4)[:, sub, :],
-                        start=(sub == 0),
-                        stop=(sub == 3),
-                    )
+                rso = tpsum.tile([P, 2 * NT], F32, tag="tp")
+                for k, part in enumerate((ssp_sb, r_sb)):
+                    for sub in range(4):
+                        nc.tensor.matmul(
+                            out=rso[:, NT * k : NT * k + NT],
+                            lhsT=fold[:, sub, :],
+                            rhs=part[:].rearrange("p (t s) -> p s t", s=4)[:, sub, :],
+                            start=(sub == 0),
+                            stop=(sub == 3),
+                        )
             alloc_codes(i)
             quant_a(i)
             if i + 1 < NT:
@@ -341,6 +387,7 @@ def tile_bgnna_kernel(tc, x, edge_index, weight, bias, out):
                 natural(i + 1)
                 special_sq(i + 1)
             quant_s(i)
+            gram_diag(i)
             if i >= 1 and (i - 1) % 4 == 3:
                 epi_v((i - 1) // 4)
             if i + 4 < NT:
@@ -348,8 +395,9 @@ def tile_bgnna_kernel(tc, x, edge_index, weight, bias, out):
         mx(NT - 1)
         epi_s(NT // 4 - 1)
 
-        nc.vector.tensor_tensor(out=rs[:], in0=rso[:], in1=resid[:], op=ALU.add)
-        nc.vector.tensor_tensor(out=ssa[:], in0=ss_raw[:], in1=css[:], op=ALU.add)
+        nc.vector.tensor_tensor(out=rs[:], in0=rso[:, NT : 2 * NT], in1=resid[:], op=ALU.add)
+        nc.vector.tensor_tensor(out=ssb[:], in0=ss_raw[:], in1=css[:], op=ALU.add)
+        nc.vector.tensor_tensor(out=ssa[:], in0=rso[:, 0:NT], in1=ssb[:], op=ALU.add)
         nc.vector.tensor_tensor(out=r2[:], in0=rs[:], in1=rs[:], op=ALU.mult)
         nc.vector.tensor_tensor(out=den[:], in0=r2[:], in1=ssa[:], op=ALU.subtract)
         nc.vector.tensor_single_scalar(out=nz[:], in_=den[:], scalar=0.0, op=ALU.not_equal)

@@ -21,16 +21,22 @@ FLOPS = 2 * N * N * C * 2 + 2 * N * C * C
 
 PIN = True
 GRAM = (3, 11, 19, 27)
-V_BANK_TILES = ()
-SEG_CAST = "G"
-SEG_SQ = "G"
+V_BANK_TILES = (1, 5)
+EBUFS = 6
+H_FIRST = 2
+H_RATE = (52, 32)
+PH1 = 28
+H_OFF = 1
+H_LAST = 2
+SEG_CAST = "V"
+SEG_SQ = "S"
 
 
 def tile_bgnna_kernel(tc, x, edge_index, weight, bias, out):
     nc = tc.nc
     with ExitStack() as ctx:
         const = ctx.enter_context(tc.tile_pool(name="const", bufs=1))
-        epool = ctx.enter_context(tc.tile_pool(name="epool", bufs=4))
+        epool = ctx.enter_context(tc.tile_pool(name="epool", bufs=EBUFS))
         gpool = ctx.enter_context(tc.tile_pool(name="gpool", bufs=3))
         cpool = ctx.enter_context(tc.tile_pool(name="cpool", bufs=3))
         work = ctx.enter_context(tc.tile_pool(name="work", bufs=2))
@@ -59,6 +65,7 @@ def tile_bgnna_kernel(tc, x, edge_index, weight, bias, out):
         nc.sync.dma_start(out=w_sb[:], in_=weight)
         load(1)
         load(2)
+        load(3)
         bias_bc = const.tile([P, C], BF16)
         nc.sync.dma_start(out=bias_bc[:], in_=bias.partition_broadcast(P))
         d_bf = const.tile([P, NT], BF16)
@@ -67,6 +74,7 @@ def tile_bgnna_kernel(tc, x, edge_index, weight, bias, out):
                 out=d_bf[:],
                 in_=edge_index.rearrange("a b -> (a b)")[0 : N * N : N + 1].rearrange("(t p) -> p t", p=P),
             )
+
 
         ident_f = const.tile([P, P], F32)
         make_identity(nc, ident_f[:])
@@ -88,14 +96,12 @@ def tile_bgnna_kernel(tc, x, edge_index, weight, bias, out):
         for sub in range(4):
             nc.vector.tensor_copy(out=fold[:, sub, 32 * sub : 32 * sub + 32], in_=gsel[:])
 
-        ss_raw = const.tile([P, NT], F32)
+        ss_raw = const.tile([P, 2 * NT], F32)
         nc.vector.memset(ss_raw[:], 0.0)
-        ss_0 = const.tile([P, 4], F32)
         ssp_sb = const.tile([P, P], F32)
         nc.vector.memset(ssp_sb[:], 0.0)
         junk = const.tile([P, N], BF16)
         tt = const.tile([P, NT * C], F32)
-        ot = const.tile([P, NT * C], F32)
         rsp = apsum.tile([P, P], F32)
         acc = {}
         grouped = {}
@@ -103,10 +109,26 @@ def tile_bgnna_kernel(tc, x, edge_index, weight, bias, out):
         banks = {}
         atmps = {}
 
-        def natural(t):
-            if t in GRAM:
-                return
-            nc.scalar.activation(out=junk[:], in_=e_tiles[t][:], func=ACT.Square, accum_out=ss_raw[:, t : t + 1])
+        halves = [(t, hf) for t in range(NT) if t not in GRAM for hf in range(2)]
+        state = {"h": 0, "load": 4}
+
+        def naturals(upto):
+            while state["h"] < min(upto, len(halves)):
+                t, hf = halves[state["h"]]
+                cs = slice(2048 * hf, 2048 * hf + 2048)
+                nc.scalar.activation(out=junk[:, cs], in_=e_tiles[t][:, cs], func=ACT.Square, accum_out=ss_raw[:, 2 * t + hf : 2 * t + hf + 1])
+                state["h"] += 1
+
+        def loads(done_tr):
+            while state["load"] < NT:
+                old = state["load"] - EBUFS
+                if old >= 0:
+                    if old > done_tr:
+                        return
+                    if old not in GRAM and halves.index((old, 1)) >= state["h"]:
+                        return
+                load(state["load"])
+                state["load"] += 1
 
         grams = {}
 
@@ -271,8 +293,8 @@ def tile_bgnna_kernel(tc, x, edge_index, weight, bias, out):
         def epi_v(b):
             nc.vector.tensor_tensor(out=tt[:, 512 * b : 512 * b + 512], in0=s2s[b][:], in1=acc[b][1][:], op=ALU.subtract)
 
-        for h in range(4):
-            nc.scalar.activation(out=junk[:, 1024 * h : 1024 * h + 1024], in_=e_0[:, 1024 * h : 1024 * h + 1024], func=ACT.Square, accum_out=ss_0[:, h : h + 1])
+        loads(0)
+        naturals(H_FIRST)
         transposes(0)
         alloc_grouped(0)
         special_a(0)
@@ -321,7 +343,6 @@ def tile_bgnna_kernel(tc, x, edge_index, weight, bias, out):
         css = const.tile([P, NT], F32)
         sq_a = const.tile([P, NT], F32)
         sq_b = const.tile([P, NT], F32)
-        s0sum = const.tile([P, 1], F32)
 
         def diag_scalars():
             nc.vector.tensor_copy(out=d32[:], in_=d_bf[:])
@@ -329,16 +350,16 @@ def tile_bgnna_kernel(tc, x, edge_index, weight, bias, out):
             nc.vector.tensor_copy(out=a1b[:], in_=a1[:])
             nc.vector.tensor_tensor(out=resid[:], in0=a1[:], in1=a1b[:], op=ALU.subtract)
             nc.vector.tensor_scalar(out=css[:], in0=d32[:], scalar1=2.0, scalar2=1.0, op0=ALU.mult, op1=ALU.add)
-            nc.vector.tensor_tensor(out=sq_a[:], in0=a1[:], in1=a1[:], op=ALU.mult)
-            nc.vector.tensor_tensor(out=sq_b[:], in0=a1b[:], in1=a1b[:], op=ALU.mult)
-            nc.vector.tensor_tensor(out=css[:, GRAM[0] : NT : 8], in0=sq_a[:, GRAM[0] : NT : 8], in1=sq_b[:, GRAM[0] : NT : 8], op=ALU.subtract)
-            nc.vector.tensor_reduce(out=s0sum[:], in_=ss_0[:], axis=AX.X, op=ALU.add)
-            nc.vector.tensor_tensor(out=css[:, 0:1], in0=css[:, 0:1], in1=s0sum[:], op=ALU.add)
+            if GRAM:
+                nc.vector.tensor_tensor(out=sq_a[:], in0=a1[:], in1=a1[:], op=ALU.mult)
+                nc.vector.tensor_tensor(out=sq_b[:], in0=a1b[:], in1=a1b[:], op=ALU.mult)
+                nc.vector.tensor_tensor(out=css[:, GRAM[0] : NT : 8], in0=sq_a[:, GRAM[0] : NT : 8], in1=sq_b[:, GRAM[0] : NT : 8], op=ALU.subtract)
 
         r_sb = const.tile([P, P], F32)
         rs = const.tile([P, NT], F32)
         ssa = const.tile([P, NT], F32)
         ssb = const.tile([P, NT], F32)
+        ssc = const.tile([P, NT], F32)
         r2 = const.tile([P, NT], F32)
         den = const.tile([P, NT], F32)
         nz = const.tile([P, NT], F32)
@@ -347,7 +368,49 @@ def tile_bgnna_kernel(tc, x, edge_index, weight, bias, out):
         rec = const.tile([P, NT], F32)
         norm = const.tile([P, NT], F32)
 
-        load(3)
+        def fold_sums(lo, hi):
+            nc.vector.tensor_copy(out=r_sb[:, 4 * lo : 4 * hi], in_=rsp[:, 4 * lo : 4 * hi])
+            rso = tpsum.tile([P, 2 * NT], F32, tag="tp")
+            for k, part in enumerate((ssp_sb, r_sb)):
+                for sub in range(4):
+                    nc.tensor.matmul(
+                        out=rso[:, NT * k + lo : NT * k + hi],
+                        lhsT=fold[:, sub, :],
+                        rhs=part[:, 4 * lo : 4 * hi].rearrange("p (t s) -> p s t", s=4)[:, sub, :],
+                        start=(sub == 0),
+                        stop=(sub == 3),
+                    )
+            return rso
+
+        def norm_chain(rso, lo, hi):
+            cs = slice(lo, hi)
+            nc.vector.tensor_tensor(out=rs[:, cs], in0=rso[:, NT + lo : NT + hi], in1=resid[:, cs], op=ALU.add)
+            nc.vector.tensor_tensor(out=ssb[:, cs], in0=ss_raw[:, 2 * lo : 2 * hi : 2], in1=ss_raw[:, 2 * lo + 1 : 2 * hi : 2], op=ALU.add)
+            nc.vector.tensor_tensor(out=r2[:, cs], in0=rs[:, cs], in1=rs[:, cs], op=ALU.mult)
+            nc.vector.tensor_tensor(out=ssc[:, cs], in0=ssb[:, cs], in1=css[:, cs], op=ALU.add)
+            nc.vector.tensor_tensor(out=ssa[:, cs], in0=rso[:, cs], in1=ssc[:, cs], op=ALU.add)
+            nc.vector.tensor_tensor(out=den[:, cs], in0=r2[:, cs], in1=ssa[:, cs], op=ALU.subtract)
+            nc.vector.tensor_single_scalar(out=nz[:, cs], in_=den[:, cs], scalar=0.0, op=ALU.not_equal)
+            nc.vector.tensor_scalar(out=pad[:, cs], in0=nz[:, cs], scalar1=-1.0, scalar2=1.0, op0=ALU.mult, op1=ALU.add)
+            nc.vector.tensor_tensor(out=dsafe[:, cs], in0=den[:, cs], in1=pad[:, cs], op=ALU.add)
+            nc.vector.reciprocal(out=rec[:, cs], in_=dsafe[:, cs])
+            nc.vector.tensor_tensor(out=norm[:, cs], in0=rec[:, cs], in1=nz[:, cs], op=ALU.mult)
+
+        out_v = out.rearrange("(t p) c -> p t c", p=P)
+
+        def finish(lo, hi):
+            for t in range(lo, hi):
+                nc.vector.scalar_tensor_tensor(
+                    out=tt[:, C * t : C * t + C],
+                    in0=tt[:, C * t : C * t + C],
+                    scalar=norm[:, t : t + 1],
+                    in1=bias_bc[:],
+                    op0=ALU.mult,
+                    op1=ALU.add,
+                )
+            nc.sync.dma_start(out=out_v[:, lo:hi, :], in_=tt[:, C * lo : C * hi].rearrange("p (t c) -> p t c", c=C))
+
+        folded = {}
         for i in range(NT):
             if i == 1:
                 xw_stage()
@@ -368,59 +431,29 @@ def tile_bgnna_kernel(tc, x, edge_index, weight, bias, out):
                 reg = bank_order(i + 1)[1:]
                 for j, h in enumerate(reg):
                     copy_bank(i + 1, h, "V" if j < nv else "S")
-            else:
-                nc.vector.tensor_copy(out=r_sb[:], in_=rsp[:])
-                rso = tpsum.tile([P, 2 * NT], F32, tag="tp")
-                for k, part in enumerate((ssp_sb, r_sb)):
-                    for sub in range(4):
-                        nc.tensor.matmul(
-                            out=rso[:, NT * k : NT * k + NT],
-                            lhsT=fold[:, sub, :],
-                            rhs=part[:].rearrange("p (t s) -> p s t", s=4)[:, sub, :],
-                            start=(sub == 0),
-                            stop=(sub == 3),
-                        )
+            if i == NT - 2:
+                folded[0] = fold_sums(0, PH1)
+            if i == NT - 1:
+                folded[1] = fold_sums(PH1, NT)
             alloc_codes(i)
             quant_a(i)
             if i + 1 < NT:
                 special_cast(i + 1)
-                natural(i + 1)
+            naturals(H_FIRST + (H_RATE[0] * max(i + H_OFF, 0)) // H_RATE[1])
+            if i + 1 < NT:
                 special_sq(i + 1)
             quant_s(i)
             gram_diag(i)
             if i >= 1 and (i - 1) % 4 == 3:
                 epi_v((i - 1) // 4)
-            if i + 4 < NT:
-                load(i + 4)
+            loads(i + 1)
         mx(NT - 1)
+        naturals(len(halves) - H_LAST)
         epi_s(NT // 4 - 1)
-
-        nc.vector.tensor_tensor(out=rs[:], in0=rso[:, NT : 2 * NT], in1=resid[:], op=ALU.add)
-        nc.vector.tensor_tensor(out=ssb[:], in0=ss_raw[:], in1=css[:], op=ALU.add)
-        nc.vector.tensor_tensor(out=ssa[:], in0=rso[:, 0:NT], in1=ssb[:], op=ALU.add)
-        nc.vector.tensor_tensor(out=r2[:], in0=rs[:], in1=rs[:], op=ALU.mult)
-        nc.vector.tensor_tensor(out=den[:], in0=r2[:], in1=ssa[:], op=ALU.subtract)
-        nc.vector.tensor_single_scalar(out=nz[:], in_=den[:], scalar=0.0, op=ALU.not_equal)
-        nc.vector.tensor_scalar(out=pad[:], in0=nz[:], scalar1=-1.0, scalar2=1.0, op0=ALU.mult, op1=ALU.add)
-        nc.vector.tensor_tensor(out=dsafe[:], in0=den[:], in1=pad[:], op=ALU.add)
-        nc.vector.reciprocal(out=rec[:], in_=dsafe[:])
-        nc.vector.tensor_tensor(out=norm[:], in0=rec[:], in1=nz[:], op=ALU.mult)
-
-        out_v = out.rearrange("(t p) c -> p t c", p=P)
-        for t in range(NT):
-            if t == NT - 4:
-                epi_v(NT // 4 - 1)
-            nc.vector.scalar_tensor_tensor(
-                out=ot[:, C * t : C * t + C],
-                in0=tt[:, C * t : C * t + C],
-                scalar=norm[:, t : t + 1],
-                in1=bias_bc[:],
-                op0=ALU.mult,
-                op1=ALU.add,
-            )
-            if t % 8 == 7 or t == NT - 5:
-                lo = 8 * (t // 8) if t % 8 == 7 and t != NT - 1 else (NT - 8 if t == NT - 5 else NT - 4)
-                nc.sync.dma_start(
-                    out=out_v[:, lo : t + 1, :],
-                    in_=ot[:, C * lo : C * (t + 1)].rearrange("p (t c) -> p t c", c=C),
-                )
+        naturals(len(halves))
+        norm_chain(folded[0], 0, PH1)
+        for lo in range(0, PH1, 8):
+            finish(lo, min(lo + 8, PH1))
+        epi_v(NT // 4 - 1)
+        norm_chain(folded[1], PH1, NT)
+        finish(PH1, NT)

@@ -16,444 +16,393 @@ P = 128
 N = 4096
 C = 128
 NT = N // P
-NG = N // 512
+PASS = 512
+NG = N // PASS
+BANK = 512
+HALF = N // 2
 FLOPS = 2 * N * N * C * 2 + 2 * N * C * C
 
-PIN = True
-GRAM = (3, 11, 19, 27)
-V_BANK_TILES = (1, 5)
-EBUFS = 6
+GRAM_STEP = 8
+GRAM_TILES = (3, 11, 19, 27)
+E_BUFS = 6
 H_FIRST = 2
-H_RATE = (52, 32)
-PH1 = 28
-H_OFF = 1
-H_LAST = 2
-SEG_CAST = "V"
-SEG_SQ = "S"
+H_TAIL = 2
+ROUND_1 = NT - 4
 
 
 def tile_bgnna_kernel(tc, x, edge_index, weight, bias, out):
     nc = tc.nc
     with ExitStack() as ctx:
         const = ctx.enter_context(tc.tile_pool(name="const", bufs=1))
-        epool = ctx.enter_context(tc.tile_pool(name="epool", bufs=EBUFS))
+        epool = ctx.enter_context(tc.tile_pool(name="epool", bufs=E_BUFS))
         gpool = ctx.enter_context(tc.tile_pool(name="gpool", bufs=3))
         cpool = ctx.enter_context(tc.tile_pool(name="cpool", bufs=3))
         work = ctx.enter_context(tc.tile_pool(name="work", bufs=2))
         tpsum = ctx.enter_context(tc.psum_pool(name="tpsum", bufs=5))
         apsum = ctx.enter_context(tc.psum_pool(name="apsum", bufs=1))
-        if PIN:
-            ctx.enter_context(tc.manual_schedule())
+        ctx.enter_context(tc.manual_schedule())
 
         e_tiles = {}
 
-        def load(t):
+        def load(t, pieces):
             e_t = epool.tile([P, N], BF16, name="e_t")
-            nc.sync.dma_start(out=e_t[:], in_=edge_index[t * P : (t + 1) * P, :])
             e_tiles[t] = e_t
+            w = N // pieces
+            for k in range(pieces):
+                nc.sync.dma_start(out=e_t[:, w * k : w * k + w], in_=edge_index[t * P : (t + 1) * P, w * k : w * k + w])
 
-        e_0 = epool.tile([P, N], BF16, name="e_t")
-        e_tiles[0] = e_0
-        for h in range(4):
-            nc.sync.dma_start(out=e_0[:, 1024 * h : 1024 * h + 1024], in_=edge_index[0:P, 1024 * h : 1024 * h + 1024])
+        load(0, 4)
         x_sb = const.tile([P, N], BF16)
         nc.sync.dma_start(
-            out=x_sb[:].rearrange("q (a r) -> q a r", a=16),
-            in_=x.rearrange("(a q e) i -> q a (e i)", a=16, q=P, e=2),
+            out=x_sb[:].rearrange("q (a r) -> q a r", a=2 * NG),
+            in_=x.rearrange("(a q e) i -> q a (e i)", a=2 * NG, q=P, e=2),
         )
         w_sb = const.tile([P, C], BF16)
         nc.sync.dma_start(out=w_sb[:], in_=weight)
-        load(1)
-        load(2)
-        load(3)
+        load(1, 1)
+        load(2, 1)
+        load(3, 1)
         bias_bc = const.tile([P, C], BF16)
         nc.sync.dma_start(out=bias_bc[:], in_=bias.partition_broadcast(P))
-        d_bf = const.tile([P, NT], BF16)
+        diag_b = const.tile([P, NT], BF16)
         with nc.allow_non_contiguous_dma(reason="the 4096 diagonal elements, one each"):
             nc.sync.dma_start(
-                out=d_bf[:],
+                out=diag_b[:],
                 in_=edge_index.rearrange("a b -> (a b)")[0 : N * N : N + 1].rearrange("(t p) -> p t", p=P),
             )
 
-
         ident_f = const.tile([P, P], F32)
         make_identity(nc, ident_f[:])
+        sq_sums = const.tile([P, 2 * NT], F32)
+        nc.gpsimd.memset(sq_sums[:], 0.0)
+        fold = const.tile([P, 4, P], F32)
+        nc.gpsimd.memset(fold[:], 0.0)
+        mask = const.tile([P, 4, PASS], BF16)
+        nc.vector.memset(mask[:], 0.0)
         ident_b = const.tile([P, P], BF16)
         nc.vector.tensor_copy(out=ident_b[:], in_=ident_f[:])
         ones_b = const.tile([P, 2], BF16)
         nc.vector.memset(ones_b[:], 1.0)
-        mask = const.tile([P, 4, 512], BF16)
-        nc.vector.memset(mask[:], 0.0)
-        for v in range(4):
-            u_t, par = v // 2, v % 2
-            mv = mask[:, v, :].rearrange("p (h e t) -> p h e t", h=64, e=2, t=4)
+
+        def build_mask(v):
+            view = mask[:, v, :].rearrange("p (h e t) -> p h e t", h=P // 2, e=2, t=4)
             for e in range(2):
-                nc.vector.tensor_copy(out=mv[:, :, e, 2 * u_t + e], in_=ident_b[:, 64 * par : 64 * par + 64])
-        gsel = const.tile([P, 32], F32)
-        nc.vector.tensor_reduce(out=gsel[:], in_=ident_f[:].rearrange("p (c t) -> p c t", t=4), axis=AX.X, op=ALU.add)
-        fold = const.tile([P, 4, P], F32)
-        nc.vector.memset(fold[:], 0.0)
-        for sub in range(4):
-            nc.vector.tensor_copy(out=fold[:, sub, 32 * sub : 32 * sub + 32], in_=gsel[:])
+                nc.vector.tensor_copy(out=view[:, :, e, 2 * (v // 2) + e], in_=ident_b[:, 64 * (v % 2) : 64 * (v % 2) + 64])
 
-        ss_raw = const.tile([P, 2 * NT], F32)
-        nc.vector.memset(ss_raw[:], 0.0)
-        ssp_sb = const.tile([P, P], F32)
-        nc.vector.memset(ssp_sb[:], 0.0)
-        junk = const.tile([P, N], BF16)
-        tt = const.tile([P, NT * C], F32)
-        rsp = apsum.tile([P, P], F32)
-        acc = {}
-        grouped = {}
-        codes = {}
+        def build_fold():
+            quarter = const.tile([P, 32], F32)
+            nc.vector.tensor_reduce(out=quarter[:], in_=ident_f[:].rearrange("p (c t) -> p c t", t=4), axis=AX.X, op=ALU.add)
+            for s in range(4):
+                nc.vector.tensor_copy(out=fold[:, s, 32 * s : 32 * s + 32], in_=quarter[:])
+
+        scrap = const.tile([P, N], BF16)
+        result = const.tile([P, NT * C], F32)
+        row_part = apsum.tile([P, 4 * NT], F32)
+        gram_part = const.tile([P, 4 * len(GRAM_TILES)], F32)
         banks = {}
-        atmps = {}
-
-        halves = [(t, hf) for t in range(NT) if t not in GRAM for hf in range(2)]
-        state = {"h": 0, "load": 4}
-
-        def naturals(upto):
-            while state["h"] < min(upto, len(halves)):
-                t, hf = halves[state["h"]]
-                cs = slice(2048 * hf, 2048 * hf + 2048)
-                nc.scalar.activation(out=junk[:, cs], in_=e_tiles[t][:, cs], func=ACT.Square, accum_out=ss_raw[:, 2 * t + hf : 2 * t + hf + 1])
-                state["h"] += 1
-
-        def loads(done_tr):
-            while state["load"] < NT:
-                old = state["load"] - EBUFS
-                if old >= 0:
-                    if old > done_tr:
-                        return
-                    if old not in GRAM and halves.index((old, 1)) >= state["h"]:
-                        return
-                load(state["load"])
-                state["load"] += 1
-
+        grouped = {}
+        exact = {}
+        codes = {}
         grams = {}
+        products = {}
+        squared = {}
 
-        def gram(t):
-            if t not in GRAM:
-                return
-            ag = grouped[t][0]
-            gr = tpsum.tile([P, 512], F32, tag="tp")
-            grams[t] = gr
-            for sub in range(4):
-                for g in range(NG):
-                    c0 = 512 * g + P * sub
-                    nc.tensor.matmul(out=gr[:, P * sub : P * sub + P], lhsT=ag[:, c0 : c0 + P], rhs=ag[:, c0 : c0 + P], start=(g == 0), stop=(g == NG - 1))
+        halves = [(t, k) for t in range(NT) if t not in GRAM_TILES for k in range(2)]
+        progress = {"halves": 0, "loads": 4}
 
-        def gram_diag(t):
-            if t not in GRAM:
-                return
-            gtmp = work.tile([P, 512], F32, name="gtmp")
-            nc.vector.tensor_tensor(
-                out=gtmp[:].rearrange("p (s m) -> p s m", s=4),
-                in0=grams[t][:].rearrange("p (s m) -> p s m", s=4),
-                in1=ident_f[:].unsqueeze(1).to_broadcast([P, 4, P]),
-                op=ALU.mult,
-            )
-            nc.vector.tensor_reduce(out=ssp_sb[:, 4 * t : 4 * t + 4], in_=gtmp[:].rearrange("p (s m) -> p s m", s=4), axis=AX.X, op=ALU.add)
+        def square_halves(upto):
+            while progress["halves"] < upto:
+                t, k = halves[progress["halves"]]
+                cols = slice(HALF * k, HALF * k + HALF)
+                nc.scalar.activation(
+                    out=scrap[:, cols], in_=e_tiles[t][:, cols], func=ACT.Square, accum_out=sq_sums[:, 2 * t + k : 2 * t + k + 1]
+                )
+                progress["halves"] += 1
+
+        def more_loads(transposed):
+            while progress["loads"] < NT:
+                old = progress["loads"] - E_BUFS
+                if old > transposed:
+                    return
+                if old >= 0 and old not in GRAM_TILES and halves.index((old, 1)) >= progress["halves"]:
+                    return
+                load(progress["loads"], 1)
+                progress["loads"] += 1
 
         def bank_order(t):
-            hs = (t // 4) // 2
-            return [hs] + [h for h in range(4) if h != hs]
+            first = (t // 4) // 2
+            return [first] + [h for h in range(4) if h != first]
 
         def transposes(t):
-            ew = e_tiles[t][:].bitcast(F32)
+            words = e_tiles[t][:].bitcast(F32)
             for h in bank_order(t):
-                tp = tpsum.tile([P, 512], F32, tag="tp")
-                for k in range(4):
-                    w0 = 512 * h + P * k
-                    nc.tensor.transpose(out=tp[:, P * k : P * k + P], in_=ew[:, w0 : w0 + P], identity=ident_f[:])
+                tp = tpsum.tile([P, BANK], F32, tag="tp")
                 banks[(t, h)] = tp
+                for k in range(4):
+                    w0 = BANK * h + P * k
+                    nc.tensor.transpose(out=tp[:, P * k : P * k + P], in_=words[:, w0 : w0 + P], identity=ident_f[:])
 
-        def alloc_grouped(t):
-            ag = gpool.tile([P, N], BF16, name="ag", align_bytes=64)
-            sg = gpool.tile([P, N], BF16, name="sg", align_bytes=64)
-            grouped[t] = (ag, sg)
+        def new_grouped(t):
+            adj_g = gpool.tile([P, N], BF16, name="adj_g", align_bytes=64)
+            sq_g = gpool.tile([P, N], BF16, name="sq_g", align_bytes=64)
+            grouped[t] = (adj_g, sq_g)
 
-        def special_a(t):
-            gs = t // 4
-            h = gs // 2
-            g2 = gs % 2
-            go = 1 - g2
-            tp = banks[(t, h)]
-            agw = grouped[t][0][:].bitcast(F32)
-            atmp = work.tile([P, 512], F32, name="atmp")
-            atmps[t] = atmp
+        def copy_bank(t, h, engine_copy):
+            engine_copy(
+                out=grouped[t][0][:].bitcast(F32)[:, BANK * h : BANK * h + BANK].rearrange("p (g i u) -> p g i u", g=2, i=P, u=2),
+                in_=banks[(t, h)][:].rearrange("p (g u i) -> p g i u", g=2, u=2, i=P),
+            )
+
+        def diagonal_bank(t):
+            g_d = t // 4
+            tp = banks[(t, g_d // 2)]
+            at = 256 * (g_d % 2)
+            other = 256 - at
+            adj_x = work.tile([P, PASS], F32, name="adj_x")
+            exact[t] = adj_x
             nc.vector.tensor_tensor(
-                out=atmp[:].rearrange("p (i u e) -> p i u e", i=P, u=2, e=2),
-                in0=tp[:].bitcast(BF16)[:, 512 * g2 : 512 * g2 + 512].rearrange("p (u i e) -> p i u e", u=2, i=P, e=2),
+                out=adj_x[:].rearrange("p (i u e) -> p i u e", i=P, u=2, e=2),
+                in0=tp[:].bitcast(BF16)[:, 2 * at : 2 * at + PASS].rearrange("p (u i e) -> p i u e", u=2, i=P, e=2),
                 in1=mask[:, t % 4, :].rearrange("p (i u e) -> p i u e", i=P, u=2, e=2),
                 op=ALU.add,
             )
+            w0 = BANK * (g_d // 2) + other
             nc.vector.tensor_copy(
-                out=agw[:, 512 * h + 256 * go : 512 * h + 256 * go + 256].rearrange("p (i u) -> p i u", i=P, u=2),
-                in_=tp[:, 256 * go : 256 * go + 256].rearrange("p (u i) -> p i u", u=2, i=P),
+                out=grouped[t][0][:].bitcast(F32)[:, w0 : w0 + 256].rearrange("p (i u) -> p i u", i=P, u=2),
+                in_=tp[:, other : other + 256].rearrange("p (u i) -> p i u", u=2, i=P),
             )
 
-        def special_cast(t):
-            gs = t // 4
-            ag = grouped[t][0]
-            dst = ag[:, 512 * gs : 512 * gs + 512]
-            if SEG_CAST == "V":
-                nc.vector.tensor_copy(out=dst, in_=atmps[t][:])
-            elif SEG_CAST == "S":
-                nc.scalar.copy(out=dst, in_=atmps[t][:])
-            else:
-                nc.gpsimd.tensor_scalar(out=dst, in0=atmps[t][:], scalar1=1.0, scalar2=0.0, op0=ALU.mult, op1=ALU.add)
+        def diagonal_adj(t):
+            nc.vector.tensor_copy(out=grouped[t][0][:, PASS * (t // 4) : PASS * (t // 4) + PASS], in_=exact[t][:])
 
-        def special_sq(t):
-            gs = t // 4
-            sg = grouped[t][1]
-            dst = sg[:, 512 * gs : 512 * gs + 512]
-            if SEG_SQ == "V":
-                nc.vector.tensor_tensor(out=dst, in0=atmps[t][:], in1=atmps[t][:], op=ALU.mult)
-            elif SEG_SQ == "S":
-                nc.scalar.activation(out=dst, in_=atmps[t][:], func=ACT.Square)
-            else:
-                nc.gpsimd.tensor_tensor(out=dst, in0=atmps[t][:], in1=atmps[t][:], op=ALU.mult)
-
-        def copy_bank(t, h, eng):
-            agw = grouped[t][0][:].bitcast(F32)
-            dst = agw[:, 512 * h : 512 * h + 512].rearrange("p (g i u) -> p g i u", g=2, i=P, u=2)
-            src = banks[(t, h)][:].rearrange("p (g u i) -> p g i u", g=2, u=2, i=P)
-            if eng == "S":
-                nc.scalar.copy(out=dst, in_=src)
-            else:
-                nc.vector.tensor_copy(out=dst, in_=src)
-
-        def v_banks(t):
-            if t == 0:
-                return 3
-            return 1 if t % 8 in V_BANK_TILES else 0
+        def diagonal_sq(t):
+            nc.scalar.activation(out=grouped[t][1][:, PASS * (t // 4) : PASS * (t // 4) + PASS], in_=exact[t][:], func=ACT.Square)
 
         def squares(t):
-            gs = t // 4
-            ag, sg = grouped[t]
-            for lo, hi in ((0, 512 * gs), (512 * gs + 512, N)):
+            adj_g, sq_g = grouped[t]
+            for lo, hi in ((0, PASS * (t // 4)), (PASS * (t // 4) + PASS, N)):
                 if hi > lo:
-                    nc.vector.tensor_tensor(out=sg[:, lo:hi], in0=ag[:, lo:hi], in1=ag[:, lo:hi], op=ALU.mult)
+                    nc.vector.tensor_tensor(out=sq_g[:, lo:hi], in0=adj_g[:, lo:hi], in1=adj_g[:, lo:hi], op=ALU.mult)
 
-        def alloc_codes(t):
+        def new_codes(t):
             a_c = cpool.tile([P, N // 4], U32, name="a_c", align_bytes=64)
             a_s = cpool.tile([P, N // 4], U8, name="a_s", align_bytes=64)
             s_c = cpool.tile([P, N // 4], U32, name="s_c", align_bytes=64)
             s_s = cpool.tile([P, N // 4], U8, name="s_s", align_bytes=64)
-            codes[t] = (a_c, a_s, s_c, s_s)
+            codes[t] = ((a_c, a_s), (s_c, s_s))
 
-        def quant_a(t):
-            a_c, a_s = codes[t][0], codes[t][1]
-            nc.vector.quantize_mx(out=a_c[:].bitcast(FP8X4), scales=a_s[:], in_=grouped[t][0][:])
+        def quantise(t, which):
+            words, scales = codes[t][which]
+            nc.vector.quantize_mx(out=words[:].bitcast(FP8X4), scales=scales[:], in_=grouped[t][which][:])
 
-        def quant_s(t):
-            s_c, s_s = codes[t][2], codes[t][3]
-            nc.vector.quantize_mx(out=s_c[:].bitcast(FP8X4), scales=s_s[:], in_=grouped[t][1][:])
-
-        def rowsum(t):
-            ag = grouped[t][0]
-            for sub in range(4):
-                col = 4 * t + sub
+        def row_sums(t):
+            adj_g = grouped[t][0]
+            for s in range(4):
                 for g in range(NG):
-                    c0 = 512 * g + P * sub
-                    nc.tensor.matmul(out=rsp[:, col : col + 1], lhsT=ag[:, c0 : c0 + P], rhs=ones_b[:, 0:1], start=(g == 0), stop=(g == NG - 1))
+                    c0 = PASS * g + P * s
+                    nc.tensor.matmul(
+                        out=row_part[:, 4 * t + s : 4 * t + s + 1], lhsT=adj_g[:, c0 : c0 + P], rhs=ones_b[:, 0:1], start=(g == 0), stop=(g == NG - 1)
+                    )
 
-        xw = {}
+        def gram(t):
+            adj_g = grouped[t][0]
+            gr = tpsum.tile([P, BANK], F32, tag="tp")
+            grams[t] = gr
+            for s in range(4):
+                for g in range(NG):
+                    c0 = PASS * g + P * s
+                    nc.tensor.matmul(
+                        out=gr[:, P * s : P * s + P], lhsT=adj_g[:, c0 : c0 + P], rhs=adj_g[:, c0 : c0 + P], start=(g == 0), stop=(g == NG - 1)
+                    )
+
+        def gram_diagonal(t):
+            kept = work.tile([P, BANK], F32, name="kept")
+            nc.vector.tensor_tensor(
+                out=kept[:].rearrange("p (s m) -> p s m", s=4),
+                in0=grams[t][:].rearrange("p (s m) -> p s m", s=4),
+                in1=ident_f[:].unsqueeze(1).to_broadcast([P, 4, P]),
+                op=ALU.mult,
+            )
+            at = 4 * GRAM_TILES.index(t)
+            nc.vector.tensor_reduce(out=gram_part[:, at : at + 4], in_=kept[:].rearrange("p (s m) -> p s m", s=4), axis=AX.X, op=ALU.add)
+
+        xw_codes = []
 
         def mx(t):
-            a_c, a_s, s_c, s_s = codes[t]
-            xg_c, xg_s, xq_c, xq_s = xw["codes"]
-            slot = t % 4
-            if slot == 0:
-                sps = apsum.tile([P, 512], F32, name="sps")
-                qps = apsum.tile([P, 512], F32, name="qps")
-                acc[t // 4] = (sps, qps)
-            sps, qps = acc[t // 4]
-            for dst, l_c, l_s, r_c, r_s in ((sps, a_c, a_s, xg_c, xg_s), (qps, s_c, s_s, xq_c, xq_s)):
+            if t % 4 == 0:
+                s_ps = apsum.tile([P, BANK], F32, name="s_ps")
+                q_ps = apsum.tile([P, BANK], F32, name="q_ps")
+                products[t // 4] = (s_ps, q_ps)
+            for which in range(2):
+                l_c, l_s = codes[t][which]
+                r_c, r_s = xw_codes[which]
                 for g in range(NG):
-                    cs = slice(P * g, P * g + P)
+                    cols = slice(P * g, P * g + P)
                     nc.tensor.matmul_mx(
-                        out=dst[:, P * slot : P * slot + P],
-                        lhsT=l_c[:, cs].bitcast(FP8X4),
-                        lhsT_scale=l_s[:, cs],
-                        rhs=r_c[:, cs].bitcast(FP8X4),
-                        rhs_scale=r_s[:, cs],
+                        out=products[t // 4][which][:, P * (t % 4) : P * (t % 4) + P],
+                        lhsT=l_c[:, cols].bitcast(FP8X4),
+                        lhsT_scale=l_s[:, cols],
+                        rhs=r_c[:, cols].bitcast(FP8X4),
+                        rhs_scale=r_s[:, cols],
                         start=(g == 0),
                         stop=(g == NG - 1),
                     )
 
-        s2s = {}
+        def square_s(b):
+            s2 = work.tile([P, BANK], F32, name="s2")
+            squared[b] = s2
+            nc.scalar.activation(out=s2[:], in_=products[b][0][:], func=ACT.Square)
 
-        def epi_s(b):
-            s2 = work.tile([P, 512], F32, name="s2")
-            s2s[b] = s2
-            nc.scalar.activation(out=s2[:], in_=acc[b][0][:], func=ACT.Square)
-
-        def epi_v(b):
-            nc.vector.tensor_tensor(out=tt[:, 512 * b : 512 * b + 512], in0=s2s[b][:], in1=acc[b][1][:], op=ALU.subtract)
-
-        loads(0)
-        naturals(H_FIRST)
-        transposes(0)
-        alloc_grouped(0)
-        special_a(0)
-        for h in bank_order(0)[1:]:
-            copy_bank(0, h, "V")
-        special_cast(0)
-        special_sq(0)
+        def minus_q(b):
+            nc.vector.tensor_tensor(out=result[:, BANK * b : BANK * b + BANK], in0=squared[b][:], in1=products[b][1][:], op=ALU.subtract)
 
         xt_sb = const.tile([P, N], BF16)
-        xg = const.tile([P, N], BF16, align_bytes=64)
-        xq = const.tile([P, N], BF16, align_bytes=64)
-        for g2 in range(NG // 2):
-            xtp = tpsum.tile([P, 1024], BF16, tag="tp")
-            for t in range(8):
-                b = 8 * g2 + t
-                nc.tensor.transpose(out=xtp[:, P * t : P * t + P], in_=x_sb[:, P * b : P * b + P], identity=ident_b[:])
-            nc.scalar.copy(out=xt_sb[:, 1024 * g2 : 1024 * g2 + 1024], in_=xtp[:])
+        xw_g = const.tile([P, N], BF16, align_bytes=64)
+        xw2_g = const.tile([P, N], BF16, align_bytes=64)
 
-        def xw_stage():
+        def x_transposed():
+            for k in range(4):
+                xtp = tpsum.tile([P, 2 * BANK], BF16, tag="tp")
+                for j in range(8):
+                    b = 8 * k + j
+                    nc.tensor.transpose(out=xtp[:, P * j : P * j + P], in_=x_sb[:, P * b : P * b + P], identity=ident_b[:])
+                nc.scalar.copy(out=xt_sb[:, 1024 * k : 1024 * k + 1024], in_=xtp[:])
+
+        def xw_quantised():
             for g in range(NG):
-                xwp = tpsum.tile([P, 512], F32, tag="tp")
+                xwp = tpsum.tile([P, BANK], F32, tag="tp")
                 for t in range(4):
                     b = 4 * g + t
                     nc.tensor.matmul(out=xwp[:, P * t : P * t + P], lhsT=xt_sb[:, P * b : P * b + P], rhs=w_sb[:], start=True, stop=True)
-                nc.vector.tensor_copy(
-                    out=xg[:, 512 * g : 512 * g + 512].rearrange("p (c t) -> p c t", t=4),
-                    in_=xwp[:].rearrange("p (t c) -> p c t", t=4),
-                )
+                cols = slice(PASS * g, PASS * g + PASS)
+                nc.vector.tensor_copy(out=xw_g[:, cols].rearrange("p (c t) -> p c t", t=4), in_=xwp[:].rearrange("p (t c) -> p c t", t=4))
                 nc.scalar.activation(
-                    out=xq[:, 512 * g : 512 * g + 512].rearrange("p (c t) -> p c t", t=4),
-                    in_=xwp[:].rearrange("p (t c) -> p c t", t=4),
-                    func=ACT.Square,
+                    out=xw2_g[:, cols].rearrange("p (c t) -> p c t", t=4), in_=xwp[:].rearrange("p (t c) -> p c t", t=4), func=ACT.Square
                 )
-            xg_c = const.tile([P, N // 4], U32, align_bytes=64)
-            xg_s = const.tile([P, N // 4], U8, align_bytes=64)
-            xq_c = const.tile([P, N // 4], U32, align_bytes=64)
-            xq_s = const.tile([P, N // 4], U8, align_bytes=64)
-            xw["codes"] = (xg_c, xg_s, xq_c, xq_s)
-            nc.vector.quantize_mx(out=xg_c[:].bitcast(FP8X4), scales=xg_s[:], in_=xg[:])
-            nc.vector.quantize_mx(out=xq_c[:].bitcast(FP8X4), scales=xq_s[:], in_=xq[:])
+            for name, src in (("xw", xw_g), ("xw2", xw2_g)):
+                words = const.tile([P, N // 4], U32, name=name + "_c", align_bytes=64)
+                scales = const.tile([P, N // 4], U8, name=name + "_s", align_bytes=64)
+                xw_codes.append((words, scales))
+                nc.vector.quantize_mx(out=words[:].bitcast(FP8X4), scales=scales[:], in_=src[:])
 
-        d32 = const.tile([P, NT], F32)
-        a1 = const.tile([P, NT], F32)
-        a1b = const.tile([P, NT], BF16)
-        resid = const.tile([P, NT], F32)
-        css = const.tile([P, NT], F32)
-        sq_a = const.tile([P, NT], F32)
-        sq_b = const.tile([P, NT], F32)
+        small = {}
+        for name in ("diag", "one_d", "rest", "extra", "sq_x", "sq_r", "rows", "rows2", "ss_a", "ss_b", "ss_c", "den", "nz", "pad", "safe", "rec", "norm"):
+            small[name] = const.tile([P, NT], F32, name=name)
+        one_d_b = const.tile([P, NT], BF16)
 
-        def diag_scalars():
-            nc.vector.tensor_copy(out=d32[:], in_=d_bf[:])
-            nc.vector.tensor_scalar_add(out=a1[:], in0=d32[:], scalar1=1.0)
-            nc.vector.tensor_copy(out=a1b[:], in_=a1[:])
-            nc.vector.tensor_tensor(out=resid[:], in0=a1[:], in1=a1b[:], op=ALU.subtract)
-            nc.vector.tensor_scalar(out=css[:], in0=d32[:], scalar1=2.0, scalar2=1.0, op0=ALU.mult, op1=ALU.add)
-            if GRAM:
-                nc.vector.tensor_tensor(out=sq_a[:], in0=a1[:], in1=a1[:], op=ALU.mult)
-                nc.vector.tensor_tensor(out=sq_b[:], in0=a1b[:], in1=a1b[:], op=ALU.mult)
-                nc.vector.tensor_tensor(out=css[:, GRAM[0] : NT : 8], in0=sq_a[:, GRAM[0] : NT : 8], in1=sq_b[:, GRAM[0] : NT : 8], op=ALU.subtract)
+        def diagonal_terms():
+            gt = slice(GRAM_TILES[0], NT, GRAM_STEP)
+            nc.vector.tensor_copy(out=small["diag"][:], in_=diag_b[:])
+            nc.vector.tensor_scalar_add(out=small["one_d"][:], in0=small["diag"][:], scalar1=1.0)
+            nc.vector.tensor_copy(out=one_d_b[:], in_=small["one_d"][:])
+            nc.vector.tensor_tensor(out=small["rest"][:], in0=small["one_d"][:], in1=one_d_b[:], op=ALU.subtract)
+            nc.vector.tensor_scalar(out=small["extra"][:], in0=small["diag"][:], scalar1=2.0, scalar2=1.0, op0=ALU.mult, op1=ALU.add)
+            nc.vector.tensor_tensor(out=small["sq_x"][:], in0=small["one_d"][:], in1=small["one_d"][:], op=ALU.mult)
+            nc.vector.tensor_tensor(out=small["sq_r"][:], in0=one_d_b[:], in1=one_d_b[:], op=ALU.mult)
+            nc.vector.tensor_tensor(out=small["extra"][:, gt], in0=small["sq_x"][:, gt], in1=small["sq_r"][:, gt], op=ALU.subtract)
 
-        r_sb = const.tile([P, P], F32)
-        rs = const.tile([P, NT], F32)
-        ssa = const.tile([P, NT], F32)
-        ssb = const.tile([P, NT], F32)
-        ssc = const.tile([P, NT], F32)
-        r2 = const.tile([P, NT], F32)
-        den = const.tile([P, NT], F32)
-        nz = const.tile([P, NT], F32)
-        pad = const.tile([P, NT], F32)
-        dsafe = const.tile([P, NT], F32)
-        rec = const.tile([P, NT], F32)
-        norm = const.tile([P, NT], F32)
+        row_sb = const.tile([P, 4 * NT], F32)
+        folded = {}
 
         def fold_sums(lo, hi):
-            nc.vector.tensor_copy(out=r_sb[:, 4 * lo : 4 * hi], in_=rsp[:, 4 * lo : 4 * hi])
-            rso = tpsum.tile([P, 2 * NT], F32, tag="tp")
-            for k, part in enumerate((ssp_sb, r_sb)):
-                for sub in range(4):
-                    nc.tensor.matmul(
-                        out=rso[:, NT * k + lo : NT * k + hi],
-                        lhsT=fold[:, sub, :],
-                        rhs=part[:, 4 * lo : 4 * hi].rearrange("p (t s) -> p s t", s=4)[:, sub, :],
-                        start=(sub == 0),
-                        stop=(sub == 3),
-                    )
-            return rso
+            nc.vector.tensor_copy(out=row_sb[:, 4 * lo : 4 * hi], in_=row_part[:, 4 * lo : 4 * hi])
+            fo = tpsum.tile([P, 2 * NT], F32, tag="tp")
+            folded[lo] = fo
+            parts = [(row_sb[:, 4 * lo : 4 * hi], fo[:, lo:hi])]
+            if lo == 0:
+                parts.append((gram_part[:], fo[:, NT : NT + len(GRAM_TILES)]))
+            for src, dst in parts:
+                for s in range(4):
+                    nc.tensor.matmul(out=dst, lhsT=fold[:, s, :], rhs=src.rearrange("p (t s) -> p s t", s=4)[:, s, :], start=(s == 0), stop=(s == 3))
 
-        def norm_chain(rso, lo, hi):
+        def norms(lo, hi):
+            fo = folded[lo]
             cs = slice(lo, hi)
-            nc.vector.tensor_tensor(out=rs[:, cs], in0=rso[:, NT + lo : NT + hi], in1=resid[:, cs], op=ALU.add)
-            nc.vector.tensor_tensor(out=ssb[:, cs], in0=ss_raw[:, 2 * lo : 2 * hi : 2], in1=ss_raw[:, 2 * lo + 1 : 2 * hi : 2], op=ALU.add)
-            nc.vector.tensor_tensor(out=r2[:, cs], in0=rs[:, cs], in1=rs[:, cs], op=ALU.mult)
-            nc.vector.tensor_tensor(out=ssc[:, cs], in0=ssb[:, cs], in1=css[:, cs], op=ALU.add)
-            nc.vector.tensor_tensor(out=ssa[:, cs], in0=rso[:, cs], in1=ssc[:, cs], op=ALU.add)
-            nc.vector.tensor_tensor(out=den[:, cs], in0=r2[:, cs], in1=ssa[:, cs], op=ALU.subtract)
-            nc.vector.tensor_single_scalar(out=nz[:, cs], in_=den[:, cs], scalar=0.0, op=ALU.not_equal)
-            nc.vector.tensor_scalar(out=pad[:, cs], in0=nz[:, cs], scalar1=-1.0, scalar2=1.0, op0=ALU.mult, op1=ALU.add)
-            nc.vector.tensor_tensor(out=dsafe[:, cs], in0=den[:, cs], in1=pad[:, cs], op=ALU.add)
-            nc.vector.reciprocal(out=rec[:, cs], in_=dsafe[:, cs])
-            nc.vector.tensor_tensor(out=norm[:, cs], in0=rec[:, cs], in1=nz[:, cs], op=ALU.mult)
+            tt = nc.vector.tensor_tensor
+            tt(out=small["rows"][:, cs], in0=fo[:, cs], in1=small["rest"][:, cs], op=ALU.add)
+            tt(out=small["ss_a"][:, cs], in0=sq_sums[:, 2 * lo : 2 * hi : 2], in1=sq_sums[:, 2 * lo + 1 : 2 * hi : 2], op=ALU.add)
+            tt(out=small["rows2"][:, cs], in0=small["rows"][:, cs], in1=small["rows"][:, cs], op=ALU.mult)
+            tt(out=small["ss_b"][:, cs], in0=small["ss_a"][:, cs], in1=small["extra"][:, cs], op=ALU.add)
+            if lo == 0:
+                gt = slice(GRAM_TILES[0], NT, GRAM_STEP)
+                tt(out=small["ss_b"][:, gt], in0=fo[:, NT : NT + len(GRAM_TILES)], in1=small["extra"][:, gt], op=ALU.add)
+            tt(out=small["den"][:, cs], in0=small["rows2"][:, cs], in1=small["ss_b"][:, cs], op=ALU.subtract)
+            nc.vector.tensor_single_scalar(out=small["nz"][:, cs], in_=small["den"][:, cs], scalar=0.0, op=ALU.not_equal)
+            nc.vector.tensor_scalar(out=small["pad"][:, cs], in0=small["nz"][:, cs], scalar1=-1.0, scalar2=1.0, op0=ALU.mult, op1=ALU.add)
+            tt(out=small["safe"][:, cs], in0=small["den"][:, cs], in1=small["pad"][:, cs], op=ALU.add)
+            nc.vector.reciprocal(out=small["rec"][:, cs], in_=small["safe"][:, cs])
+            tt(out=small["norm"][:, cs], in0=small["rec"][:, cs], in1=small["nz"][:, cs], op=ALU.mult)
 
-        out_v = out.rearrange("(t p) c -> p t c", p=P)
+        out_tiles = out.rearrange("(t p) c -> p t c", p=P)
 
         def finish(lo, hi):
             for t in range(lo, hi):
+                cols = slice(C * t, C * t + C)
                 nc.vector.scalar_tensor_tensor(
-                    out=tt[:, C * t : C * t + C],
-                    in0=tt[:, C * t : C * t + C],
-                    scalar=norm[:, t : t + 1],
-                    in1=bias_bc[:],
-                    op0=ALU.mult,
-                    op1=ALU.add,
+                    out=result[:, cols], in0=result[:, cols], scalar=small["norm"][:, t : t + 1], in1=bias_bc[:], op0=ALU.mult, op1=ALU.add
                 )
-            nc.sync.dma_start(out=out_v[:, lo:hi, :], in_=tt[:, C * lo : C * hi].rearrange("p (t c) -> p t c", c=C))
+            nc.sync.dma_start(out=out_tiles[:, lo:hi, :], in_=result[:, C * lo : C * hi].rearrange("p (t c) -> p t c", c=C))
 
-        folded = {}
+        more_loads(0)
+        square_halves(H_FIRST)
+        build_mask(0)
+        transposes(0)
+        new_grouped(0)
+        diagonal_bank(0)
+        for h in bank_order(0)[1:]:
+            copy_bank(0, h, nc.vector.tensor_copy)
+        diagonal_adj(0)
+        diagonal_sq(0)
+        for v in range(1, 4):
+            build_mask(v)
+        build_fold()
+        x_transposed()
+
+        in_stream = len(halves) - H_FIRST - H_TAIL
         for i in range(NT):
+            nxt = i + 1
             if i == 1:
-                xw_stage()
-                diag_scalars()
-            if i + 1 < NT:
-                transposes(i + 1)
+                xw_quantised()
+                diagonal_terms()
+            if nxt < NT:
+                transposes(nxt)
             if i >= 1:
                 mx(i - 1)
-                if (i - 1) % 4 == 3:
-                    epi_s((i - 1) // 4)
-            rowsum(i)
-            gram(i)
+                if i % 4 == 0:
+                    square_s(i // 4 - 1)
+            row_sums(i)
+            if i in GRAM_TILES:
+                gram(i)
             squares(i)
-            if i + 1 < NT:
-                alloc_grouped(i + 1)
-                special_a(i + 1)
-                nv = v_banks(i + 1)
-                reg = bank_order(i + 1)[1:]
-                for j, h in enumerate(reg):
-                    copy_bank(i + 1, h, "V" if j < nv else "S")
+            if nxt < NT:
+                new_grouped(nxt)
+                diagonal_bank(nxt)
+                for h in bank_order(nxt)[1:]:
+                    copy_bank(nxt, h, nc.scalar.copy)
             if i == NT - 2:
-                folded[0] = fold_sums(0, PH1)
+                fold_sums(0, ROUND_1)
             if i == NT - 1:
-                folded[1] = fold_sums(PH1, NT)
-            alloc_codes(i)
-            quant_a(i)
-            if i + 1 < NT:
-                special_cast(i + 1)
-            naturals(H_FIRST + (H_RATE[0] * max(i + H_OFF, 0)) // H_RATE[1])
-            if i + 1 < NT:
-                special_sq(i + 1)
-            quant_s(i)
-            gram_diag(i)
-            if i >= 1 and (i - 1) % 4 == 3:
-                epi_v((i - 1) // 4)
-            loads(i + 1)
+                fold_sums(ROUND_1, NT)
+            new_codes(i)
+            quantise(i, 0)
+            if nxt < NT:
+                diagonal_adj(nxt)
+            square_halves(H_FIRST + (in_stream * nxt) // NT)
+            if nxt < NT:
+                diagonal_sq(nxt)
+            quantise(i, 1)
+            if i in GRAM_TILES:
+                gram_diagonal(i)
+            if i >= 1 and i % 4 == 0:
+                minus_q(i // 4 - 1)
+            more_loads(nxt)
+
         mx(NT - 1)
-        naturals(len(halves) - H_LAST)
-        epi_s(NT // 4 - 1)
-        naturals(len(halves))
-        norm_chain(folded[0], 0, PH1)
-        for lo in range(0, PH1, 8):
-            finish(lo, min(lo + 8, PH1))
-        epi_v(NT // 4 - 1)
-        norm_chain(folded[1], PH1, NT)
-        finish(PH1, NT)
+        square_s(NT // 4 - 1)
+        square_halves(len(halves))
+        norms(0, ROUND_1)
+        for lo in range(0, ROUND_1, 8):
+            finish(lo, min(lo + 8, ROUND_1))
+        minus_q(NT // 4 - 1)
+        norms(ROUND_1, NT)
+        finish(ROUND_1, NT)

@@ -345,7 +345,9 @@ def tile_bgnna_kernel(tc, x, edge_index, weight, bias, out):
 
         more_loads(0)
         square_halves(H_FIRST)
-        build_mask(0)
+        for v in range(4):
+            build_mask(v)
+        build_fold()
         transposes(0)
         new_grouped(0)
         diagonal_bank(0)
@@ -353,9 +355,6 @@ def tile_bgnna_kernel(tc, x, edge_index, weight, bias, out):
             copy_bank(0, h, nc.vector.tensor_copy)
         diagonal_adj(0)
         diagonal_sq(0)
-        for v in range(1, 4):
-            build_mask(v)
-        build_fold()
         x_transposed()
 
         in_stream = len(halves) - H_FIRST - H_TAIL

@@ -365,11 +365,14 @@ def tile_bgnna_kernel(tc, x, edge_index, weight, bias, out):
                 diagonal_terms()
             if nxt < NT:
                 transposes(nxt)
+            else:
+                row_sums(i)
             if i >= 1:
                 mx(i - 1)
                 if i % 4 == 0:
                     square_s(i // 4 - 1)
-            row_sums(i)
+            if nxt < NT:
+                row_sums(i)
             if i in GRAM_TILES:
                 gram(i)
             squares(i)

@@ -18,8 +18,13 @@ C = 128
 NT = N // P
 PASS = 512
 NG = N // PASS
+PACK = 4
+PASS_PAIRS = PASS // 2
 BANK = 512
 HALF = N // 2
+QUARTER = P // PACK
+TILE_BANKS = N // 2 // BANK
+QUAD = 4
 FLOPS = 2 * N * N * C * 2 + 2 * N * C * C
 
 GRAM_STEP = 8
@@ -27,7 +32,8 @@ GRAM_TILES = (3, 11, 19, 27)
 E_BUFS = 6
 H_FIRST = 2
 H_TAIL = 2
-ROUND_1 = NT - 4
+ROUND_1 = NT - QUAD
+STORE_TILES = 8
 
 
 def tile_bgnna_kernel(tc, x, edge_index, weight, bias, out):
@@ -47,15 +53,16 @@ def tile_bgnna_kernel(tc, x, edge_index, weight, bias, out):
         def load(t, pieces):
             e_t = epool.tile([P, N], BF16, name="e_t")
             e_tiles[t] = e_t
-            w = N // pieces
-            for k in range(pieces):
-                nc.sync.dma_start(out=e_t[:, w * k : w * k + w], in_=edge_index[t * P : (t + 1) * P, w * k : w * k + w])
+            width = N // pieces
+            for piece in range(pieces):
+                cols = slice(width * piece, width * piece + width)
+                nc.sync.dma_start(out=e_t[:, cols], in_=edge_index[t * P : (t + 1) * P, cols])
 
-        load(0, 4)
+        load(0, TILE_BANKS)
         x_sb = const.tile([P, N], BF16)
         nc.sync.dma_start(
-            out=x_sb[:].rearrange("q (a r) -> q a r", a=2 * NG),
-            in_=x.rearrange("(a q e) i -> q a (e i)", a=2 * NG, q=P, e=2),
+            out=x_sb[:].rearrange("p (a e c) -> p a (e c)", a=2 * NG, e=2, c=C),
+            in_=x.rearrange("(a p e) c -> p a (e c)", a=2 * NG, p=P, e=2),
         )
         w_sb = const.tile([P, C], BF16)
         nc.sync.dma_start(out=w_sb[:], in_=weight)
@@ -68,16 +75,16 @@ def tile_bgnna_kernel(tc, x, edge_index, weight, bias, out):
         with nc.allow_non_contiguous_dma(reason="the 4096 diagonal elements, one each"):
             nc.sync.dma_start(
                 out=diag_b[:],
-                in_=edge_index.rearrange("a b -> (a b)")[0 : N * N : N + 1].rearrange("(t p) -> p t", p=P),
+                in_=edge_index.rearrange("y z -> (y z)")[0 : N * N : N + 1].rearrange("(t p) -> p t", p=P),
             )
 
         ident_f = const.tile([P, P], F32)
         make_identity(nc, ident_f[:])
         sq_sums = const.tile([P, 2 * NT], F32)
         nc.gpsimd.memset(sq_sums[:], 0.0)
-        fold = const.tile([P, 4, P], F32)
+        fold = const.tile([P, PACK, P], F32)
         nc.gpsimd.memset(fold[:], 0.0)
-        mask = const.tile([P, 4, PASS], BF16)
+        mask = const.tile([P, QUAD, PASS], BF16)
         nc.vector.memset(mask[:], 0.0)
         ident_b = const.tile([P, P], BF16)
         nc.vector.tensor_copy(out=ident_b[:], in_=ident_f[:])
@@ -85,20 +92,21 @@ def tile_bgnna_kernel(tc, x, edge_index, weight, bias, out):
         nc.vector.memset(ones_b[:], 1.0)
 
         def build_mask(v):
-            view = mask[:, v, :].rearrange("p (h e t) -> p h e t", h=P // 2, e=2, t=4)
+            view = mask[:, v, :].rearrange("p (w e j) -> p w e j", w=P // 2, e=2, j=PACK)
+            col = (P // 2) * (v % 2)
             for e in range(2):
-                nc.vector.tensor_copy(out=view[:, :, e, 2 * (v // 2) + e], in_=ident_b[:, 64 * (v % 2) : 64 * (v % 2) + 64])
+                nc.vector.tensor_copy(out=view[:, :, e, 2 * (v // 2) + e], in_=ident_b[:, col : col + P // 2])
 
         def build_fold():
-            quarter = const.tile([P, 32], F32)
-            nc.vector.tensor_reduce(out=quarter[:], in_=ident_f[:].rearrange("p (c t) -> p c t", t=4), axis=AX.X, op=ALU.add)
-            for s in range(4):
-                nc.vector.tensor_copy(out=fold[:, s, 32 * s : 32 * s + 32], in_=quarter[:])
+            quarter = const.tile([P, QUARTER], F32)
+            nc.vector.tensor_reduce(out=quarter[:], in_=ident_f[:].rearrange("p (r j) -> p r j", j=PACK), axis=AX.X, op=ALU.add)
+            for q in range(PACK):
+                nc.vector.tensor_copy(out=fold[:, q, QUARTER * q : QUARTER * q + QUARTER], in_=quarter[:])
 
         scrap = const.tile([P, N], BF16)
         result = const.tile([P, NT * C], F32)
-        row_part = apsum.tile([P, 4 * NT], F32)
-        gram_part = const.tile([P, 4 * len(GRAM_TILES)], F32)
+        row_part = apsum.tile([P, PACK * NT], F32)
+        gram_part = const.tile([P, PACK * len(GRAM_TILES)], F32)
         banks = {}
         grouped = {}
         exact = {}
@@ -107,15 +115,15 @@ def tile_bgnna_kernel(tc, x, edge_index, weight, bias, out):
         products = {}
         squared = {}
 
-        halves = [(t, k) for t in range(NT) if t not in GRAM_TILES for k in range(2)]
+        halves = [(t, half) for t in range(NT) if t not in GRAM_TILES for half in range(2)]
         progress = {"halves": 0, "loads": 4}
 
         def square_halves(upto):
             while progress["halves"] < upto:
-                t, k = halves[progress["halves"]]
-                cols = slice(HALF * k, HALF * k + HALF)
+                t, half = halves[progress["halves"]]
+                cols = slice(HALF * half, HALF * half + HALF)
                 nc.scalar.activation(
-                    out=scrap[:, cols], in_=e_tiles[t][:, cols], func=ACT.Square, accum_out=sq_sums[:, 2 * t + k : 2 * t + k + 1]
+                    out=scrap[:, cols], in_=e_tiles[t][:, cols], func=ACT.Square, accum_out=sq_sums[:, 2 * t + half : 2 * t + half + 1]
                 )
                 progress["halves"] += 1
 
@@ -130,17 +138,17 @@ def tile_bgnna_kernel(tc, x, edge_index, weight, bias, out):
                 progress["loads"] += 1
 
         def bank_order(t):
-            first = (t // 4) // 2
-            return [first] + [h for h in range(4) if h != first]
+            first = (t // QUAD) // 2
+            return [first] + [h for h in range(TILE_BANKS) if h != first]
 
         def transposes(t):
-            words = e_tiles[t][:].bitcast(F32)
+            pairs = e_tiles[t][:].bitcast(F32)
             for h in bank_order(t):
                 tp = tpsum.tile([P, BANK], F32, tag="tp")
                 banks[(t, h)] = tp
-                for k in range(4):
-                    w0 = BANK * h + P * k
-                    nc.tensor.transpose(out=tp[:, P * k : P * k + P], in_=words[:, w0 : w0 + P], identity=ident_f[:])
+                for plane in range(BANK // P):
+                    pair0 = BANK * h + P * plane
+                    nc.tensor.transpose(out=tp[:, P * plane : P * plane + P], in_=pairs[:, pair0 : pair0 + P], identity=ident_f[:])
 
         def new_grouped(t):
             adj_g = gpool.tile([P, N], BF16, name="adj_g", align_bytes=64)
@@ -154,42 +162,44 @@ def tile_bgnna_kernel(tc, x, edge_index, weight, bias, out):
             )
 
         def diagonal_bank(t):
-            g_d = t // 4
+            g_d = t // QUAD
             tp = banks[(t, g_d // 2)]
-            at = 256 * (g_d % 2)
-            other = 256 - at
+            at = PASS_PAIRS * (g_d % 2)
+            other = PASS_PAIRS - at
             adj_x = work.tile([P, PASS], F32, name="adj_x")
             exact[t] = adj_x
             nc.vector.tensor_tensor(
                 out=adj_x[:].rearrange("p (i u e) -> p i u e", i=P, u=2, e=2),
                 in0=tp[:].bitcast(BF16)[:, 2 * at : 2 * at + PASS].rearrange("p (u i e) -> p i u e", u=2, i=P, e=2),
-                in1=mask[:, t % 4, :].rearrange("p (i u e) -> p i u e", i=P, u=2, e=2),
+                in1=mask[:, t % QUAD, :].rearrange("p (i u e) -> p i u e", i=P, u=2, e=2),
                 op=ALU.add,
             )
-            w0 = BANK * (g_d // 2) + other
+            pair0 = BANK * (g_d // 2) + other
             nc.vector.tensor_copy(
-                out=grouped[t][0][:].bitcast(F32)[:, w0 : w0 + 256].rearrange("p (i u) -> p i u", i=P, u=2),
-                in_=tp[:, other : other + 256].rearrange("p (u i) -> p i u", u=2, i=P),
+                out=grouped[t][0][:].bitcast(F32)[:, pair0 : pair0 + PASS_PAIRS].rearrange("p (i u) -> p i u", i=P, u=2),
+                in_=tp[:, other : other + PASS_PAIRS].rearrange("p (u i) -> p i u", u=2, i=P),
             )
 
         def diagonal_adj(t):
-            nc.vector.tensor_copy(out=grouped[t][0][:, PASS * (t // 4) : PASS * (t // 4) + PASS], in_=exact[t][:])
+            c0 = PASS * (t // QUAD)
+            nc.vector.tensor_copy(out=grouped[t][0][:, c0 : c0 + PASS], in_=exact[t][:])
 
         def diagonal_sq(t):
-            nc.scalar.activation(out=grouped[t][1][:, PASS * (t // 4) : PASS * (t // 4) + PASS], in_=exact[t][:], func=ACT.Square)
+            c0 = PASS * (t // QUAD)
+            nc.scalar.activation(out=grouped[t][1][:, c0 : c0 + PASS], in_=exact[t][:], func=ACT.Square)
 
         def squares(t):
             adj_g, sq_g = grouped[t]
-            for lo, hi in ((0, PASS * (t // 4)), (PASS * (t // 4) + PASS, N)):
-                if hi > lo:
-                    nc.vector.tensor_tensor(out=sq_g[:, lo:hi], in0=adj_g[:, lo:hi], in1=adj_g[:, lo:hi], op=ALU.mult)
+            for c0, c1 in ((0, PASS * (t // QUAD)), (PASS * (t // QUAD) + PASS, N)):
+                if c1 > c0:
+                    nc.vector.tensor_tensor(out=sq_g[:, c0:c1], in0=adj_g[:, c0:c1], in1=adj_g[:, c0:c1], op=ALU.mult)
 
         def new_codes(t):
-            a_c = cpool.tile([P, N // 4], U32, name="a_c", align_bytes=64)
-            a_s = cpool.tile([P, N // 4], U8, name="a_s", align_bytes=64)
-            s_c = cpool.tile([P, N // 4], U32, name="s_c", align_bytes=64)
-            s_s = cpool.tile([P, N // 4], U8, name="s_s", align_bytes=64)
-            codes[t] = ((a_c, a_s), (s_c, s_s))
+            adj_c = cpool.tile([P, N // PACK], U32, name="adj_c", align_bytes=64)
+            adj_s = cpool.tile([P, N // PACK], U8, name="adj_s", align_bytes=64)
+            sq_c = cpool.tile([P, N // PACK], U32, name="sq_c", align_bytes=64)
+            sq_s = cpool.tile([P, N // PACK], U8, name="sq_s", align_bytes=64)
+            codes[t] = ((adj_c, adj_s), (sq_c, sq_s))
 
         def quantise(t, which):
             words, scales = codes[t][which]
@@ -197,49 +207,53 @@ def tile_bgnna_kernel(tc, x, edge_index, weight, bias, out):
 
         def row_sums(t):
             adj_g = grouped[t][0]
-            for s in range(4):
+            for q in range(PACK):
                 for g in range(NG):
-                    c0 = PASS * g + P * s
+                    c0 = PASS * g + P * q
                     nc.tensor.matmul(
-                        out=row_part[:, 4 * t + s : 4 * t + s + 1], lhsT=adj_g[:, c0 : c0 + P], rhs=ones_b[:, 0:1], start=(g == 0), stop=(g == NG - 1)
+                        out=row_part[:, PACK * t + q : PACK * t + q + 1],
+                        lhsT=adj_g[:, c0 : c0 + P],
+                        rhs=ones_b[:, 0:1],
+                        start=(g == 0),
+                        stop=(g == NG - 1),
                     )
 
         def gram(t):
             adj_g = grouped[t][0]
             gr = tpsum.tile([P, BANK], F32, tag="tp")
             grams[t] = gr
-            for s in range(4):
+            for q in range(PACK):
                 for g in range(NG):
-                    c0 = PASS * g + P * s
+                    c0 = PASS * g + P * q
                     nc.tensor.matmul(
-                        out=gr[:, P * s : P * s + P], lhsT=adj_g[:, c0 : c0 + P], rhs=adj_g[:, c0 : c0 + P], start=(g == 0), stop=(g == NG - 1)
+                        out=gr[:, P * q : P * q + P], lhsT=adj_g[:, c0 : c0 + P], rhs=adj_g[:, c0 : c0 + P], start=(g == 0), stop=(g == NG - 1)
                     )
 
         def gram_diagonal(t):
             kept = work.tile([P, BANK], F32, name="kept")
             nc.vector.tensor_tensor(
-                out=kept[:].rearrange("p (s m) -> p s m", s=4),
-                in0=grams[t][:].rearrange("p (s m) -> p s m", s=4),
-                in1=ident_f[:].unsqueeze(1).to_broadcast([P, 4, P]),
+                out=kept[:].rearrange("p (q m) -> p q m", q=PACK),
+                in0=grams[t][:].rearrange("p (q m) -> p q m", q=PACK),
+                in1=ident_f[:].unsqueeze(1).to_broadcast([P, PACK, P]),
                 op=ALU.mult,
             )
-            at = 4 * GRAM_TILES.index(t)
-            nc.vector.tensor_reduce(out=gram_part[:, at : at + 4], in_=kept[:].rearrange("p (s m) -> p s m", s=4), axis=AX.X, op=ALU.add)
+            col = PACK * GRAM_TILES.index(t)
+            nc.vector.tensor_reduce(out=gram_part[:, col : col + PACK], in_=kept[:].rearrange("p (q m) -> p q m", q=PACK), axis=AX.X, op=ALU.add)
 
         xw_codes = []
 
         def mx(t):
-            if t % 4 == 0:
-                s_ps = apsum.tile([P, BANK], F32, name="s_ps")
-                q_ps = apsum.tile([P, BANK], F32, name="q_ps")
-                products[t // 4] = (s_ps, q_ps)
+            if t % QUAD == 0:
+                first_ps = apsum.tile([P, BANK], F32, name="first_ps")
+                second_ps = apsum.tile([P, BANK], F32, name="second_ps")
+                products[t // QUAD] = (first_ps, second_ps)
             for which in range(2):
                 l_c, l_s = codes[t][which]
                 r_c, r_s = xw_codes[which]
                 for g in range(NG):
                     cols = slice(P * g, P * g + P)
                     nc.tensor.matmul_mx(
-                        out=products[t // 4][which][:, P * (t % 4) : P * (t % 4) + P],
+                        out=products[t // QUAD][which][:, P * (t % QUAD) : P * (t % QUAD) + P],
                         lhsT=l_c[:, cols].bitcast(FP8X4),
                         lhsT_scale=l_s[:, cols],
                         rhs=r_c[:, cols].bitcast(FP8X4),
@@ -248,50 +262,51 @@ def tile_bgnna_kernel(tc, x, edge_index, weight, bias, out):
                         stop=(g == NG - 1),
                     )
 
-        def square_s(b):
-            s2 = work.tile([P, BANK], F32, name="s2")
-            squared[b] = s2
-            nc.scalar.activation(out=s2[:], in_=products[b][0][:], func=ACT.Square)
+        def square_first(quad):
+            first_sq = work.tile([P, BANK], F32, name="first_sq")
+            squared[quad] = first_sq
+            nc.scalar.activation(out=first_sq[:], in_=products[quad][0][:], func=ACT.Square)
 
-        def minus_q(b):
-            nc.vector.tensor_tensor(out=result[:, BANK * b : BANK * b + BANK], in0=squared[b][:], in1=products[b][1][:], op=ALU.subtract)
+        def minus_second(quad):
+            nc.vector.tensor_tensor(out=result[:, BANK * quad : BANK * quad + BANK], in0=squared[quad][:], in1=products[quad][1][:], op=ALU.subtract)
 
         xt_sb = const.tile([P, N], BF16)
         xw_g = const.tile([P, N], BF16, align_bytes=64)
         xw2_g = const.tile([P, N], BF16, align_bytes=64)
 
         def x_transposed():
-            for k in range(4):
+            per_bank = 2 * BANK // P
+            for bank in range(NT // per_bank):
                 xtp = tpsum.tile([P, 2 * BANK], BF16, tag="tp")
-                for j in range(8):
-                    b = 8 * k + j
-                    nc.tensor.transpose(out=xtp[:, P * j : P * j + P], in_=x_sb[:, P * b : P * b + P], identity=ident_b[:])
-                nc.scalar.copy(out=xt_sb[:, 1024 * k : 1024 * k + 1024], in_=xtp[:])
+                for slot in range(per_bank):
+                    blk = per_bank * bank + slot
+                    nc.tensor.transpose(out=xtp[:, P * slot : P * slot + P], in_=x_sb[:, P * blk : P * blk + P], identity=ident_b[:])
+                nc.scalar.copy(out=xt_sb[:, 2 * BANK * bank : 2 * BANK * bank + 2 * BANK], in_=xtp[:])
 
         def xw_quantised():
             for g in range(NG):
                 xwp = tpsum.tile([P, BANK], F32, tag="tp")
-                for t in range(4):
-                    b = 4 * g + t
-                    nc.tensor.matmul(out=xwp[:, P * t : P * t + P], lhsT=xt_sb[:, P * b : P * b + P], rhs=w_sb[:], start=True, stop=True)
+                for j in range(PACK):
+                    blk = PACK * g + j
+                    nc.tensor.matmul(out=xwp[:, P * j : P * j + P], lhsT=xt_sb[:, P * blk : P * blk + P], rhs=w_sb[:], start=True, stop=True)
                 cols = slice(PASS * g, PASS * g + PASS)
-                nc.vector.tensor_copy(out=xw_g[:, cols].rearrange("p (c t) -> p c t", t=4), in_=xwp[:].rearrange("p (t c) -> p c t", t=4))
+                nc.vector.tensor_copy(out=xw_g[:, cols].rearrange("p (c j) -> p c j", j=PACK), in_=xwp[:].rearrange("p (j c) -> p c j", j=PACK))
                 nc.scalar.activation(
-                    out=xw2_g[:, cols].rearrange("p (c t) -> p c t", t=4), in_=xwp[:].rearrange("p (t c) -> p c t", t=4), func=ACT.Square
+                    out=xw2_g[:, cols].rearrange("p (c j) -> p c j", j=PACK), in_=xwp[:].rearrange("p (j c) -> p c j", j=PACK), func=ACT.Square
                 )
             for name, src in (("xw", xw_g), ("xw2", xw2_g)):
-                words = const.tile([P, N // 4], U32, name=name + "_c", align_bytes=64)
-                scales = const.tile([P, N // 4], U8, name=name + "_s", align_bytes=64)
+                words = const.tile([P, N // PACK], U32, name=name + "_c", align_bytes=64)
+                scales = const.tile([P, N // PACK], U8, name=name + "_s", align_bytes=64)
                 xw_codes.append((words, scales))
                 nc.vector.quantize_mx(out=words[:].bitcast(FP8X4), scales=scales[:], in_=src[:])
 
         small = {}
-        for name in ("diag", "one_d", "rest", "extra", "sq_x", "sq_r", "rows", "rows2", "ss_a", "ss_b", "ss_c", "den", "nz", "pad", "safe", "rec", "norm"):
+        for name in ("diag", "one_d", "rest", "extra", "sq_x", "sq_r", "rows", "rows2", "ss_a", "ss_b", "den", "nz", "pad", "safe", "rec", "norm"):
             small[name] = const.tile([P, NT], F32, name=name)
         one_d_b = const.tile([P, NT], BF16)
+        gram_cols = slice(GRAM_TILES[0], NT, GRAM_STEP)
 
         def diagonal_terms():
-            gt = slice(GRAM_TILES[0], NT, GRAM_STEP)
             nc.vector.tensor_copy(out=small["diag"][:], in_=diag_b[:])
             nc.vector.tensor_scalar_add(out=small["one_d"][:], in0=small["diag"][:], scalar1=1.0)
             nc.vector.tensor_copy(out=one_d_b[:], in_=small["one_d"][:])
@@ -299,21 +314,25 @@ def tile_bgnna_kernel(tc, x, edge_index, weight, bias, out):
             nc.vector.tensor_scalar(out=small["extra"][:], in0=small["diag"][:], scalar1=2.0, scalar2=1.0, op0=ALU.mult, op1=ALU.add)
             nc.vector.tensor_tensor(out=small["sq_x"][:], in0=small["one_d"][:], in1=small["one_d"][:], op=ALU.mult)
             nc.vector.tensor_tensor(out=small["sq_r"][:], in0=one_d_b[:], in1=one_d_b[:], op=ALU.mult)
-            nc.vector.tensor_tensor(out=small["extra"][:, gt], in0=small["sq_x"][:, gt], in1=small["sq_r"][:, gt], op=ALU.subtract)
+            nc.vector.tensor_tensor(
+                out=small["extra"][:, gram_cols], in0=small["sq_x"][:, gram_cols], in1=small["sq_r"][:, gram_cols], op=ALU.subtract
+            )
 
-        row_sb = const.tile([P, 4 * NT], F32)
+        row_sb = const.tile([P, PACK * NT], F32)
         folded = {}
 
         def fold_sums(lo, hi):
-            nc.vector.tensor_copy(out=row_sb[:, 4 * lo : 4 * hi], in_=row_part[:, 4 * lo : 4 * hi])
+            nc.vector.tensor_copy(out=row_sb[:, PACK * lo : PACK * hi], in_=row_part[:, PACK * lo : PACK * hi])
             fo = tpsum.tile([P, 2 * NT], F32, tag="tp")
             folded[lo] = fo
-            parts = [(row_sb[:, 4 * lo : 4 * hi], fo[:, lo:hi])]
+            parts = [(row_sb[:, PACK * lo : PACK * hi], fo[:, lo:hi])]
             if lo == 0:
                 parts.append((gram_part[:], fo[:, NT : NT + len(GRAM_TILES)]))
             for src, dst in parts:
-                for s in range(4):
-                    nc.tensor.matmul(out=dst, lhsT=fold[:, s, :], rhs=src.rearrange("p (t s) -> p s t", s=4)[:, s, :], start=(s == 0), stop=(s == 3))
+                for q in range(PACK):
+                    nc.tensor.matmul(
+                        out=dst, lhsT=fold[:, q, :], rhs=src.rearrange("p (t q) -> p q t", q=PACK)[:, q, :], start=(q == 0), stop=(q == PACK - 1)
+                    )
 
         def norms(lo, hi):
             fo = folded[lo]
@@ -324,8 +343,7 @@ def tile_bgnna_kernel(tc, x, edge_index, weight, bias, out):
             tt(out=small["rows2"][:, cs], in0=small["rows"][:, cs], in1=small["rows"][:, cs], op=ALU.mult)
             tt(out=small["ss_b"][:, cs], in0=small["ss_a"][:, cs], in1=small["extra"][:, cs], op=ALU.add)
             if lo == 0:
-                gt = slice(GRAM_TILES[0], NT, GRAM_STEP)
-                tt(out=small["ss_b"][:, gt], in0=fo[:, NT : NT + len(GRAM_TILES)], in1=small["extra"][:, gt], op=ALU.add)
+                tt(out=small["ss_b"][:, gram_cols], in0=fo[:, NT : NT + len(GRAM_TILES)], in1=small["extra"][:, gram_cols], op=ALU.add)
             tt(out=small["den"][:, cs], in0=small["rows2"][:, cs], in1=small["ss_b"][:, cs], op=ALU.subtract)
             nc.vector.tensor_single_scalar(out=small["nz"][:, cs], in_=small["den"][:, cs], scalar=0.0, op=ALU.not_equal)
             nc.vector.tensor_scalar(out=small["pad"][:, cs], in0=small["nz"][:, cs], scalar1=-1.0, scalar2=1.0, op0=ALU.mult, op1=ALU.add)
@@ -345,7 +363,7 @@ def tile_bgnna_kernel(tc, x, edge_index, weight, bias, out):
 
         more_loads(0)
         square_halves(H_FIRST)
-        for v in range(4):
+        for v in range(QUAD):
             build_mask(v)
         build_fold()
         transposes(0)
@@ -358,53 +376,53 @@ def tile_bgnna_kernel(tc, x, edge_index, weight, bias, out):
         x_transposed()
 
         in_stream = len(halves) - H_FIRST - H_TAIL
-        for i in range(NT):
-            nxt = i + 1
-            if i == 1:
+        for step in range(NT):
+            nxt = step + 1
+            if step == 1:
                 xw_quantised()
                 diagonal_terms()
             if nxt < NT:
                 transposes(nxt)
             else:
-                row_sums(i)
-            if i >= 1:
-                mx(i - 1)
-                if i % 4 == 0:
-                    square_s(i // 4 - 1)
+                row_sums(step)
+            if step >= 1:
+                mx(step - 1)
+                if step % QUAD == 0:
+                    square_first(step // QUAD - 1)
             if nxt < NT:
-                row_sums(i)
-            if i in GRAM_TILES:
-                gram(i)
-            squares(i)
+                row_sums(step)
+            if step in GRAM_TILES:
+                gram(step)
+            squares(step)
             if nxt < NT:
                 new_grouped(nxt)
                 diagonal_bank(nxt)
                 for h in bank_order(nxt)[1:]:
                     copy_bank(nxt, h, nc.scalar.copy)
-            if i == NT - 2:
+            if step == NT - 2:
                 fold_sums(0, ROUND_1)
-            if i == NT - 1:
+            if step == NT - 1:
                 fold_sums(ROUND_1, NT)
-            new_codes(i)
-            quantise(i, 0)
+            new_codes(step)
+            quantise(step, 0)
             if nxt < NT:
                 diagonal_adj(nxt)
             square_halves(H_FIRST + (in_stream * nxt) // NT)
             if nxt < NT:
                 diagonal_sq(nxt)
-            quantise(i, 1)
-            if i in GRAM_TILES:
-                gram_diagonal(i)
-            if i >= 1 and i % 4 == 0:
-                minus_q(i // 4 - 1)
+            quantise(step, 1)
+            if step in GRAM_TILES:
+                gram_diagonal(step)
+            if step >= 1 and step % QUAD == 0:
+                minus_second(step // QUAD - 1)
             more_loads(nxt)
 
         mx(NT - 1)
-        square_s(NT // 4 - 1)
+        square_first(NT // QUAD - 1)
         square_halves(len(halves))
         norms(0, ROUND_1)
-        for lo in range(0, ROUND_1, 8):
-            finish(lo, min(lo + 8, ROUND_1))
-        minus_q(NT // 4 - 1)
+        for lo in range(0, ROUND_1, STORE_TILES):
+            finish(lo, min(lo + STORE_TILES, ROUND_1))
+        minus_second(NT // QUAD - 1)
         norms(ROUND_1, NT)
         finish(ROUND_1, NT)

from contextlib import ExitStack

import concourse.mybir as mybir
from concourse.masks import make_identity

F32 = mybir.dt.float32
BF16 = mybir.dt.bfloat16
U32 = mybir.dt.uint32
U8 = mybir.dt.uint8
FP8X4 = mybir.dt.float8_e4m3fn_x4
ALU = mybir.AluOpType
ACT = mybir.ActivationFunctionType
AX = mybir.AxisListType

P = 128
N = 4096
C = 128
NT = N // P
PASS = 512
NG = N // PASS
PACK = 4
PASS_PAIRS = PASS // 2
BANK = 512
HALF = N // 2
QUARTER = P // PACK
TILE_BANKS = N // 2 // BANK
QUAD = 4
FLOPS = 2 * N * N * C * 2 + 2 * N * C * C

GRAM_STEP = 8
GRAM_TILES = (3, 11, 19, 27)
E_BUFS = 6
H_FIRST = 2
H_TAIL = 2
ROUND_1 = NT - QUAD
STORE_TILES = 8


def tile_bgnna_kernel(tc, x, edge_index, weight, bias, out):
    nc = tc.nc
    with ExitStack() as ctx:
        const = ctx.enter_context(tc.tile_pool(name="const", bufs=1))
        epool = ctx.enter_context(tc.tile_pool(name="epool", bufs=E_BUFS))
        gpool = ctx.enter_context(tc.tile_pool(name="gpool", bufs=3))
        cpool = ctx.enter_context(tc.tile_pool(name="cpool", bufs=3))
        work = ctx.enter_context(tc.tile_pool(name="work", bufs=2))
        tpsum = ctx.enter_context(tc.psum_pool(name="tpsum", bufs=5))
        apsum = ctx.enter_context(tc.psum_pool(name="apsum", bufs=1))
        ctx.enter_context(tc.manual_schedule())

        e_tiles = {}

        def load(t, pieces):
            e_t = epool.tile([P, N], BF16, name="e_t")
            e_tiles[t] = e_t
            width = N // pieces
            for piece in range(pieces):
                cols = slice(width * piece, width * piece + width)
                nc.sync.dma_start(out=e_t[:, cols], in_=edge_index[t * P : (t + 1) * P, cols])

        load(0, TILE_BANKS)
        x_sb = const.tile([P, N], BF16)
        nc.sync.dma_start(
            out=x_sb[:].rearrange("p (a e c) -> p a (e c)", a=2 * NG, e=2, c=C),
            in_=x.rearrange("(a p e) c -> p a (e c)", a=2 * NG, p=P, e=2),
        )
        w_sb = const.tile([P, C], BF16)
        nc.sync.dma_start(out=w_sb[:], in_=weight)
        load(1, 1)
        load(2, 1)
        load(3, 1)
        bias_bc = const.tile([P, C], BF16)
        nc.sync.dma_start(out=bias_bc[:], in_=bias.partition_broadcast(P))
        diag_b = const.tile([P, NT], BF16)
        with nc.allow_non_contiguous_dma(reason="the 4096 diagonal elements, one each"):
            nc.sync.dma_start(
                out=diag_b[:],
                in_=edge_index.rearrange("y z -> (y z)")[0 : N * N : N + 1].rearrange("(t p) -> p t", p=P),
            )

        ident_f = const.tile([P, P], F32)
        make_identity(nc, ident_f[:])
        sq_sums = const.tile([P, 2 * NT], F32)
        nc.gpsimd.memset(sq_sums[:], 0.0)
        fold = const.tile([P, PACK, P], F32)
        nc.gpsimd.memset(fold[:], 0.0)
        mask = const.tile([P, QUAD, PASS], BF16)
        nc.vector.memset(mask[:], 0.0)
        ident_b = const.tile([P, P], BF16)
        nc.vector.tensor_copy(out=ident_b[:], in_=ident_f[:])
        ones_b = const.tile([P, 2], BF16)
        nc.vector.memset(ones_b[:], 1.0)

        def build_mask(v):
            view = mask[:, v, :].rearrange("p (w e j) -> p w e j", w=P // 2, e=2, j=PACK)
            col = (P // 2) * (v % 2)
            for e in range(2):
                nc.vector.tensor_copy(out=view[:, :, e, 2 * (v // 2) + e], in_=ident_b[:, col : col + P // 2])

        def build_fold():
            quarter = const.tile([P, QUARTER], F32)
            nc.vector.tensor_reduce(out=quarter[:], in_=ident_f[:].rearrange("p (r j) -> p r j", j=PACK), axis=AX.X, op=ALU.add)
            for q in range(PACK):
                nc.vector.tensor_copy(out=fold[:, q, QUARTER * q : QUARTER * q + QUARTER], in_=quarter[:])

        scrap = const.tile([P, N], BF16)
        result = const.tile([P, NT * C], F32)
        row_part = apsum.tile([P, PACK * NT], F32)
        gram_part = const.tile([P, PACK * len(GRAM_TILES)], F32)
        banks = {}
        grouped = {}
        exact = {}
        codes = {}
        grams = {}
        products = {}
        squared = {}

        halves = [(t, half) for t in range(NT) if t not in GRAM_TILES for half in range(2)]
        progress = {"halves": 0, "loads": 4}

        def square_halves(upto):
            while progress["halves"] < upto:
                t, half = halves[progress["halves"]]
                cols = slice(HALF * half, HALF * half + HALF)
                nc.scalar.activation(
                    out=scrap[:, cols], in_=e_tiles[t][:, cols], func=ACT.Square, accum_out=sq_sums[:, 2 * t + half : 2 * t + half + 1]
                )
                progress["halves"] += 1

        def more_loads(transposed):
            while progress["loads"] < NT:
                old = progress["loads"] - E_BUFS
                if old > transposed:
                    return
                if old >= 0 and old not in GRAM_TILES and halves.index((old, 1)) >= progress["halves"]:
                    return
                load(progress["loads"], 1)
                progress["loads"] += 1

        def bank_order(t):
            first = (t // QUAD) // 2
            return [first] + [h for h in range(TILE_BANKS) if h != first]

        def transposes(t):
            pairs = e_tiles[t][:].bitcast(F32)
            for h in bank_order(t):
                tp = tpsum.tile([P, BANK], F32, tag="tp")
                banks[(t, h)] = tp
                for plane in range(BANK // P):
                    pair0 = BANK * h + P * plane
                    nc.tensor.transpose(out=tp[:, P * plane : P * plane + P], in_=pairs[:, pair0 : pair0 + P], identity=ident_f[:])

        def new_grouped(t):
            adj_g = gpool.tile([P, N], BF16, name="adj_g", align_bytes=64)
            sq_g = gpool.tile([P, N], BF16, name="sq_g", align_bytes=64)
            grouped[t] = (adj_g, sq_g)

        def copy_bank(t, h, engine_copy):
            engine_copy(
                out=grouped[t][0][:].bitcast(F32)[:, BANK * h : BANK * h + BANK].rearrange("p (g i u) -> p g i u", g=2, i=P, u=2),
                in_=banks[(t, h)][:].rearrange("p (g u i) -> p g i u", g=2, u=2, i=P),
            )

        def diagonal_bank(t):
            g_d = t // QUAD
            tp = banks[(t, g_d // 2)]
            at = PASS_PAIRS * (g_d % 2)
            other = PASS_PAIRS - at
            adj_x = work.tile([P, PASS], F32, name="adj_x")
            exact[t] = adj_x
            nc.vector.tensor_tensor(
                out=adj_x[:].rearrange("p (i u e) -> p i u e", i=P, u=2, e=2),
                in0=tp[:].bitcast(BF16)[:, 2 * at : 2 * at + PASS].rearrange("p (u i e) -> p i u e", u=2, i=P, e=2),
                in1=mask[:, t % QUAD, :].rearrange("p (i u e) -> p i u e", i=P, u=2, e=2),
                op=ALU.add,
            )
            pair0 = BANK * (g_d // 2) + other
            nc.vector.tensor_copy(
                out=grouped[t][0][:].bitcast(F32)[:, pair0 : pair0 + PASS_PAIRS].rearrange("p (i u) -> p i u", i=P, u=2),
                in_=tp[:, other : other + PASS_PAIRS].rearrange("p (u i) -> p i u", u=2, i=P),
            )

        def diagonal_adj(t):
            c0 = PASS * (t // QUAD)
            nc.vector.tensor_copy(out=grouped[t][0][:, c0 : c0 + PASS], in_=exact[t][:])

        def diagonal_sq(t):
            c0 = PASS * (t // QUAD)
            nc.scalar.activation(out=grouped[t][1][:, c0 : c0 + PASS], in_=exact[t][:], func=ACT.Square)

        def squares(t):
            adj_g, sq_g = grouped[t]
            for c0, c1 in ((0, PASS * (t // QUAD)), (PASS * (t // QUAD) + PASS, N)):
                if c1 > c0:
                    nc.vector.tensor_tensor(out=sq_g[:, c0:c1], in0=adj_g[:, c0:c1], in1=adj_g[:, c0:c1], op=ALU.mult)

        def new_codes(t):
            adj_c = cpool.tile([P, N // PACK], U32, name="adj_c", align_bytes=64)
            adj_s = cpool.tile([P, N // PACK], U8, name="adj_s", align_bytes=64)
            sq_c = cpool.tile([P, N // PACK], U32, name="sq_c", align_bytes=64)
            sq_s = cpool.tile([P, N // PACK], U8, name="sq_s", align_bytes=64)
            codes[t] = ((adj_c, adj_s), (sq_c, sq_s))

        def quantise(t, which):
            words, scales = codes[t][which]
            nc.vector.quantize_mx(out=words[:].bitcast(FP8X4), scales=scales[:], in_=grouped[t][which][:])

        def row_sums(t):
            adj_g = grouped[t][0]
            for q in range(PACK):
                for g in range(NG):
                    c0 = PASS * g + P * q
                    nc.tensor.matmul(
                        out=row_part[:, PACK * t + q : PACK * t + q + 1],
                        lhsT=adj_g[:, c0 : c0 + P],
                        rhs=ones_b[:, 0:1],
                        start=(g == 0),
                        stop=(g == NG - 1),
                    )

        def gram(t):
            adj_g = grouped[t][0]
            gr = tpsum.tile([P, BANK], F32, tag="tp")
            grams[t] = gr
            for q in range(PACK):
                for g in range(NG):
                    c0 = PASS * g + P * q
                    nc.tensor.matmul(
                        out=gr[:, P * q : P * q + P], lhsT=adj_g[:, c0 : c0 + P], rhs=adj_g[:, c0 : c0 + P], start=(g == 0), stop=(g == NG - 1)
                    )

        def gram_diagonal(t):
            kept = work.tile([P, BANK], F32, name="kept")
            nc.vector.tensor_tensor(
                out=kept[:].rearrange("p (q m) -> p q m", q=PACK),
                in0=grams[t][:].rearrange("p (q m) -> p q m", q=PACK),
                in1=ident_f[:].unsqueeze(1).to_broadcast([P, PACK, P]),
                op=ALU.mult,
            )
            col = PACK * GRAM_TILES.index(t)
            nc.vector.tensor_reduce(out=gram_part[:, col : col + PACK], in_=kept[:].rearrange("p (q m) -> p q m", q=PACK), axis=AX.X, op=ALU.add)

        xw_codes = []

        def mx(t):
            if t % QUAD == 0:
                first_ps = apsum.tile([P, BANK], F32, name="first_ps")
                second_ps = apsum.tile([P, BANK], F32, name="second_ps")
                products[t // QUAD] = (first_ps, second_ps)
            for which in range(2):
                l_c, l_s = codes[t][which]
                r_c, r_s = xw_codes[which]
                for g in range(NG):
                    cols = slice(P * g, P * g + P)
                    nc.tensor.matmul_mx(
                        out=products[t // QUAD][which][:, P * (t % QUAD) : P * (t % QUAD) + P],
                        lhsT=l_c[:, cols].bitcast(FP8X4),
                        lhsT_scale=l_s[:, cols],
                        rhs=r_c[:, cols].bitcast(FP8X4),
                        rhs_scale=r_s[:, cols],
                        start=(g == 0),
                        stop=(g == NG - 1),
                    )

        def square_first(quad):
            first_sq = work.tile([P, BANK], F32, name="first_sq")
            squared[quad] = first_sq
            nc.scalar.activation(out=first_sq[:], in_=products[quad][0][:], func=ACT.Square)

        def minus_second(quad):
            nc.vector.tensor_tensor(out=result[:, BANK * quad : BANK * quad + BANK], in0=squared[quad][:], in1=products[quad][1][:], op=ALU.subtract)

        xt_sb = const.tile([P, N], BF16)
        xw_g = const.tile([P, N], BF16, align_bytes=64)
        xw2_g = const.tile([P, N], BF16, align_bytes=64)

        def x_transposed():
            per_bank = 2 * BANK // P
            for bank in range(NT // per_bank):
                xtp = tpsum.tile([P, 2 * BANK], BF16, tag="tp")
                for slot in range(per_bank):
                    blk = per_bank * bank + slot
                    nc.tensor.transpose(out=xtp[:, P * slot : P * slot + P], in_=x_sb[:, P * blk : P * blk + P], identity=ident_b[:])
                nc.scalar.copy(out=xt_sb[:, 2 * BANK * bank : 2 * BANK * bank + 2 * BANK], in_=xtp[:])

        def xw_quantised():
            for g in range(NG):
                xwp = tpsum.tile([P, BANK], F32, tag="tp")
                for j in range(PACK):
                    blk = PACK * g + j
                    nc.tensor.matmul(out=xwp[:, P * j : P * j + P], lhsT=xt_sb[:, P * blk : P * blk + P], rhs=w_sb[:], start=True, stop=True)
                cols = slice(PASS * g, PASS * g + PASS)
                nc.vector.tensor_copy(out=xw_g[:, cols].rearrange("p (c j) -> p c j", j=PACK), in_=xwp[:].rearrange("p (j c) -> p c j", j=PACK))
                nc.scalar.activation(
                    out=xw2_g[:, cols].rearrange("p (c j) -> p c j", j=PACK), in_=xwp[:].rearrange("p (j c) -> p c j", j=PACK), func=ACT.Square
                )
            for name, src in (("xw", xw_g), ("xw2", xw2_g)):
                words = const.tile([P, N // PACK], U32, name=name + "_c", align_bytes=64)
                scales = const.tile([P, N // PACK], U8, name=name + "_s", align_bytes=64)
                xw_codes.append((words, scales))
                nc.vector.quantize_mx(out=words[:].bitcast(FP8X4), scales=scales[:], in_=src[:])

        small = {}
        for name in ("diag", "one_d", "rest", "extra", "sq_x", "sq_r", "rows", "rows2", "ss_a", "ss_b", "den", "nz", "pad", "safe", "rec", "norm"):
            small[name] = const.tile([P, NT], F32, name=name)
        one_d_b = const.tile([P, NT], BF16)
        gram_cols = slice(GRAM_TILES[0], NT, GRAM_STEP)

        def diagonal_terms():
            nc.vector.tensor_copy(out=small["diag"][:], in_=diag_b[:])
            nc.vector.tensor_scalar_add(out=small["one_d"][:], in0=small["diag"][:], scalar1=1.0)
            nc.vector.tensor_copy(out=one_d_b[:], in_=small["one_d"][:])
            nc.vector.tensor_tensor(out=small["rest"][:], in0=small["one_d"][:], in1=one_d_b[:], op=ALU.subtract)
            nc.vector.tensor_scalar(out=small["extra"][:], in0=small["diag"][:], scalar1=2.0, scalar2=1.0, op0=ALU.mult, op1=ALU.add)
            nc.vector.tensor_tensor(out=small["sq_x"][:], in0=small["one_d"][:], in1=small["one_d"][:], op=ALU.mult)
            nc.vector.tensor_tensor(out=small["sq_r"][:], in0=one_d_b[:], in1=one_d_b[:], op=ALU.mult)
            nc.vector.tensor_tensor(
                out=small["extra"][:, gram_cols], in0=small["sq_x"][:, gram_cols], in1=small["sq_r"][:, gram_cols], op=ALU.subtract
            )

        row_sb = const.tile([P, PACK * NT], F32)
        folded = {}

        def fold_sums(lo, hi):
            nc.vector.tensor_copy(out=row_sb[:, PACK * lo : PACK * hi], in_=row_part[:, PACK * lo : PACK * hi])
            fo = tpsum.tile([P, 2 * NT], F32, tag="tp")
            folded[lo] = fo
            parts = [(row_sb[:, PACK * lo : PACK * hi], fo[:, lo:hi])]
            if lo == 0:
                parts.append((gram_part[:], fo[:, NT : NT + len(GRAM_TILES)]))
            for src, dst in parts:
                for q in range(PACK):
                    nc.tensor.matmul(
                        out=dst, lhsT=fold[:, q, :], rhs=src.rearrange("p (t q) -> p q t", q=PACK)[:, q, :], start=(q == 0), stop=(q == PACK - 1)
                    )

        def norms(lo, hi):
            fo = folded[lo]
            cs = slice(lo, hi)
            tt = nc.vector.tensor_tensor
            tt(out=small["rows"][:, cs], in0=fo[:, cs], in1=small["rest"][:, cs], op=ALU.add)
            tt(out=small["ss_a"][:, cs], in0=sq_sums[:, 2 * lo : 2 * hi : 2], in1=sq_sums[:, 2 * lo + 1 : 2 * hi : 2], op=ALU.add)
            tt(out=small["rows2"][:, cs], in0=small["rows"][:, cs], in1=small["rows"][:, cs], op=ALU.mult)
            tt(out=small["ss_b"][:, cs], in0=small["ss_a"][:, cs], in1=small["extra"][:, cs], op=ALU.add)
            if lo == 0:
                tt(out=small["ss_b"][:, gram_cols], in0=fo[:, NT : NT + len(GRAM_TILES)], in1=small["extra"][:, gram_cols], op=ALU.add)
            tt(out=small["den"][:, cs], in0=small["rows2"][:, cs], in1=small["ss_b"][:, cs], op=ALU.subtract)
            nc.vector.tensor_single_scalar(out=small["nz"][:, cs], in_=small["den"][:, cs], scalar=0.0, op=ALU.not_equal)
            nc.vector.tensor_scalar(out=small["pad"][:, cs], in0=small["nz"][:, cs], scalar1=-1.0, scalar2=1.0, op0=ALU.mult, op1=ALU.add)
            tt(out=small["safe"][:, cs], in0=small["den"][:, cs], in1=small["pad"][:, cs], op=ALU.add)
            nc.vector.reciprocal(out=small["rec"][:, cs], in_=small["safe"][:, cs])
            tt(out=small["norm"][:, cs], in0=small["rec"][:, cs], in1=small["nz"][:, cs], op=ALU.mult)

        out_tiles = out.rearrange("(t p) c -> p t c", p=P)

        def finish(lo, hi):
            for t in range(lo, hi):
                cols = slice(C * t, C * t + C)
                nc.vector.scalar_tensor_tensor(
                    out=result[:, cols], in0=result[:, cols], scalar=small["norm"][:, t : t + 1], in1=bias_bc[:], op0=ALU.mult, op1=ALU.add
                )
            nc.sync.dma_start(out=out_tiles[:, lo:hi, :], in_=result[:, C * lo : C * hi].rearrange("p (t c) -> p t c", c=C))

        more_loads(0)
        square_halves(H_FIRST)
        for v in range(QUAD):
            build_mask(v)
        build_fold()
        transposes(0)
        new_grouped(0)
        diagonal_bank(0)
        for h in bank_order(0)[1:]:
            copy_bank(0, h, nc.vector.tensor_copy)
        diagonal_adj(0)
        diagonal_sq(0)
        x_transposed()

        in_stream = len(halves) - H_FIRST - H_TAIL
        for step in range(NT):
            nxt = step + 1
            if step == 1:
                xw_quantised()
                diagonal_terms()
            if nxt < NT:
                transposes(nxt)
            else:
                row_sums(step)
            if step >= 1:
                mx(step - 1)
                if step % QUAD == 0:
                    square_first(step // QUAD - 1)
            if nxt < NT:
                row_sums(step)
            if step in GRAM_TILES:
                gram(step)
            squares(step)
            if nxt < NT:
                new_grouped(nxt)
                diagonal_bank(nxt)
                for h in bank_order(nxt)[1:]:
                    copy_bank(nxt, h, nc.scalar.copy)
            if step == NT - 2:
                fold_sums(0, ROUND_1)
            if step == NT - 1:
                fold_sums(ROUND_1, NT)
            new_codes(step)
            quantise(step, 0)
            if nxt < NT:
                diagonal_adj(nxt)
            square_halves(H_FIRST + (in_stream * nxt) // NT)
            if nxt < NT:
                diagonal_sq(nxt)
            quantise(step, 1)
            if step in GRAM_TILES:
                gram_diagonal(step)
            if step >= 1 and step % QUAD == 0:
                minus_second(step // QUAD - 1)
            more_loads(nxt)

        mx(NT - 1)
        square_first(NT // QUAD - 1)
        square_halves(len(halves))
        norms(0, ROUND_1)
        for lo in range(0, ROUND_1, STORE_TILES):
            finish(lo, min(lo + STORE_TILES, ROUND_1))
        minus_second(NT // QUAD - 1)
        norms(ROUND_1, NT)
        finish(ROUND_1, NT)
